import numpy as np
import ml_dtypes


def mxq(x, axis, fmt="e4m3"):
    dtype, down = {"e4m3": (ml_dtypes.float8_e4m3fn, 7), "e5m2": (ml_dtypes.float8_e5m2, 14)}[fmt]
    v = np.moveaxis(np.asarray(x, np.float32).astype(ml_dtypes.bfloat16).astype(np.float64), axis, -1)
    blocks = v.reshape(v.shape[:-1] + (-1, 32))
    amax = np.abs(blocks).max(-1, keepdims=True)
    byte = np.maximum(np.where(amax > 0, np.frexp(amax)[1] - 1 + 127, 0) - down, 1)
    scale = np.exp2(byte - 127.0)
    codes = (blocks / scale).astype(np.float32).astype(dtype).astype(np.float64)
    return np.moveaxis((codes * scale).reshape(v.shape), -1, axis)


WIDE = False


def mx_kscale(k):
    if not WIDE:
        return np.ones(k)
    levels = np.array([10, -10, 5, -5, 0])
    if k % 512:
        return np.exp2(np.random.permutation(np.resize(levels, k // 32))).repeat(32)
    a = np.empty((k // 512, 16))
    for p in range(k // 512):
        a[p, :8] = np.random.permutation(np.resize(levels, 8))
        for g in range(8):
            far = levels[np.abs(levels - a[p, g]) >= 10]
            a[p, g + 8] = far[np.random.randint(len(far))]
    return np.exp2(a.ravel()).repeat(32)


BF16 = ml_dtypes.bfloat16


def bf(x):
    return np.asarray(x, np.float32).astype(BF16)


def f64(x):
    return np.asarray(x).astype(np.float64)


LQ, LK, D, H, DK, DV = 1024, 1024, 2048, 4, 128, 128
HV = H * DV
LN_EPS = 1e-5


def setup_inputs():
    s = mx_kscale(HV)
    return {"attn_out": bf(np.random.standard_normal((H, LQ, DV)) * 0.7 * s.reshape(H, DV)[:, None, :]),
            "residual": bf(np.random.standard_normal((LQ, D))),
            "proj_w": bf(np.random.standard_normal((HV, D)) / np.sqrt(HV) / s[:, None]),
            "proj_b": bf(np.random.standard_normal(D) * 0.3),
            "ln_g": bf(1.0 + 0.1 * np.random.standard_normal(D)),
            "ln_b": bf(0.1 * np.random.standard_normal(D))}


def core(attn_out, residual, proj_w, proj_b, ln_g, ln_b):
    x = f64(attn_out).transpose(1, 0, 2).reshape(LQ, HV)
    y = (mxq(x, 1, "e4m3") @ mxq(f64(proj_w), 0, "e4m3")) + f64(proj_b) + f64(residual)
    mu = y.mean(-1, keepdims=True)
    var = ((y - mu) ** 2).mean(-1, keepdims=True)
    return (y - mu) / np.sqrt(var + LN_EPS) * f64(ln_g) + f64(ln_b)


def e4m3fn_bytes(y):
    return np.clip(np.asarray(y, np.float64), -448.0, 448.0).astype(np.float32).astype(ml_dtypes.float8_e4m3fn).view(np.uint8)


def reference(attn_out, residual, proj_w, proj_b, ln_g, ln_b):
    out = core(attn_out, residual, proj_w, proj_b, ln_g, ln_b)
    s = np.max(np.abs(out)) / 448.0
    return out, e4m3fn_bytes(out / s)

@@ -1,0 +1,277 @@
+from contextlib import ExitStack
+
+import concourse.mybir as mybir
+from concourse.masks import make_identity
+
+F32 = mybir.dt.float32
+BF16 = mybir.dt.bfloat16
+U32 = mybir.dt.uint32
+U8 = mybir.dt.uint8
+FP8X4 = mybir.dt.float8_e4m3fn_x4
+FP8 = mybir.dt.float8_e4m3fn
+ALU = mybir.AluOpType
+ACT = mybir.ActivationFunctionType
+AX = mybir.AxisListType
+
+P = 128
+LQ = 1024
+D = 2048
+H = 4
+DV = 128
+K = H * DV
+NT = LQ // P
+CH = 512
+NCH = D // CH
+LN_EPS = 1e-5
+FLOPS = 2 * LQ * K * D
+
+CAST_V = 1344
+NB = 2
+NQ = NT // NB
+NJ = D // P
+N_ON_GPSIMD = (0, 0, 0, 0, 0, 0, 0, 0)
+CPO_ON_VECTOR = (0, 1, 0, 0, 0, 1, 0, 0)
+B_PIECES = (4, 4, 1, 1, 1, 1, 1, 1)
+
+
+def tile_multiheadattention_pb_kernel(tc, attn_out, residual, proj_w, proj_b, ln_g, ln_b, out_0, out_1):
+    nc = tc.nc
+    with ExitStack() as ctx:
+        keep = ctx.enter_context(tc.tile_pool(name="keep", bufs=1))
+        work = ctx.enter_context(tc.tile_pool(name="work", bufs=6))
+        psum = ctx.enter_context(tc.psum_pool(name="psum", bufs=3))
+
+        x_view = attn_out.rearrange("h (p i) j -> i p h j", i=NT)
+        w_view = proj_w.rearrange("(p j) w -> p j w", j=4)
+        r_view = residual.rearrange("(p i) d -> i p d", i=NT)
+        o0_view = out_0.rearrange("(p i) d -> i p d", i=NT)
+        o1_view = out_1.rearrange("(p i) d -> i p d", i=NT)
+
+        x_sb = []
+        for i in range(NT):
+            x_sb.append(keep.tile([P, H, DV], BF16, name="x_sb%d" % i))
+        r_sb = []
+        for i in range(NT):
+            r_sb.append(keep.tile([P, D], BF16, name="r_sb%d" % i))
+        b_bc = keep.tile([P, D], BF16, name="b_bc")
+        gb_rows = keep.tile([P, P], BF16, name="gb_rows")
+        o_sb = []
+        for i in range(NT):
+            o_sb.append(keep.tile([P, D], F32, name="o_sb%d" % i))
+
+        ident = keep.tile([P, P], F32, name="ident")
+        ident_b = keep.tile([P, P], BF16, name="ident_b")
+        ones_b = keep.tile([P, P], BF16, name="ones_b")
+        ones = keep.tile([P, 1], F32, name="ones")
+        zeros = keep.tile([P, 1], F32, name="zeros")
+        warm = keep.tile([P, 1], F32, name="warm")
+        sums = keep.tile([P, NT, NCH], F32, name="sums")
+        sums_s = keep.tile([P, NT, NCH], F32, name="sums_s")
+        negmu = keep.tile([P, NT], F32, name="negmu")
+        ssq = keep.tile([P, NT], F32, name="ssq")
+        sd = keep.tile([P, NT], F32, name="sd")
+        rstd = keep.tile([P, NT], F32, name="rstd")
+        am = keep.tile([P, NT * NCH], F32, name="am")
+        gb_col = keep.tile([P, 2 * NJ], F32, name="gb_col")
+
+        x_codes = {}
+        x_scales = {}
+        w_codes = []
+        w_scales = []
+
+        def prepare_x(a):
+            xt = psum.tile([P, 2, 2, P], F32, name="xt", tag="t2")
+            for e in range(2):
+                words = x_sb[2 * a + e][:].rearrange("p h j -> p (h j)").bitcast(F32)
+                for u in range(2):
+                    nc.tensor.transpose(xt[:, e, u, :], words[:, u::2], ident[:])
+            xg = keep.tile([P, 2 * P * 4], BF16, name="xg%d" % a, align_bytes=64)
+            dst = xg[:].bitcast(F32).rearrange("p (e r u) -> p e r u", e=2, u=2)
+            src = xt[:].rearrange("p e u r -> p e r u")
+            if a == 0:
+                nc.vector.tensor_copy(out=dst, in_=src)
+            else:
+                nc.scalar.copy(out=dst, in_=src)
+            xc = keep.tile([P, 2 * P], U32, name="x_codes%d" % a, align_bytes=64)
+            xs = keep.tile([P, 2 * P], U8, name="x_scales%d" % a, align_bytes=64)
+            nc.vector.quantize_mx(out=xc[:].bitcast(FP8X4), scales=xs[:], in_=xg[:])
+            x_codes[a] = xc
+            x_scales[a] = xs
+
+        with tc.tile_pool(name="wpool", bufs=1) as wpool:
+            w_raw = []
+            for c in range(NCH):
+                w_raw.append(wpool.tile([P, 4, CH], BF16, name="w_raw%d" % c))
+            b_row = wpool.tile([P, D], BF16, name="b_row")
+
+            nc.vector.memset(b_row[:], 0.0)
+            nc.vector.memset(ones_b[:], 1.0)
+            nc.vector.memset(gb_rows[:], 0.0)
+            nc.vector.memset(ones[:], 1.0)
+            nc.vector.memset(zeros[:], 0.0)
+            make_identity(nc, ident[:])
+            make_identity(nc, ident_b[:])
+            nc.scalar.activation(out=warm[:], in_=ones[:], func=ACT.Sqrt)
+
+            for i in (0, 1):
+                nc.sync.dma_start(out=x_sb[i][:], in_=x_view[i])
+            nc.sync.dma_start(out=b_row[0:1, :], in_=proj_b.rearrange("(o d) -> o d", o=1))
+            nc.sync.dma_start(out=r_sb[0][:], in_=r_view[0])
+            for c in range(NCH):
+                nc.sync.dma_start(out=w_raw[c][:], in_=w_view[:, :, c * CH:(c + 1) * CH])
+            nc.sync.dma_start(out=r_sb[1][:], in_=r_view[1])
+            nc.sync.dma_start(out=gb_rows[0:NJ, :], in_=ln_g.rearrange("(j p) -> j p", p=P))
+            nc.sync.dma_start(out=gb_rows[NJ:2 * NJ, :], in_=ln_b.rearrange("(j p) -> j p", p=P))
+            for a in range(1, NT // 2):
+                for e in range(2):
+                    nc.sync.dma_start(out=x_sb[2 * a + e][:], in_=x_view[2 * a + e])
+                for e in range(2):
+                    nc.sync.dma_start(out=r_sb[2 * a + e][:], in_=r_view[2 * a + e])
+
+            prepare_x(0)
+
+            for c in range(NCH):
+                cs = slice(c * CH, (c + 1) * CH)
+                pb = psum.tile([P, CH], F32, name="pb", tag="t1")
+                nc.tensor.matmul(out=pb[:], lhsT=ones_b[:], rhs=b_row[:, cs], start=True, stop=True)
+                nc.scalar.copy(out=b_bc[:, cs], in_=pb[:])
+
+            for c in range(NCH):
+                wg = wpool.tile([P, CH, 4], BF16, name="wg%d" % c, align_bytes=64)
+                src = w_raw[c][:].rearrange("p j w -> p w j")
+                if c in (1, 2):
+                    nc.scalar.copy(out=wg[:], in_=src)
+                else:
+                    nc.vector.tensor_copy(out=wg[:], in_=src)
+                wc = keep.tile([P, CH], U32, name="w_codes%d" % c, align_bytes=64)
+                ws = keep.tile([P, CH], U8, name="w_scales%d" % c, align_bytes=64)
+                nc.vector.quantize_mx(out=wc[:].bitcast(FP8X4), scales=ws[:], in_=wg[:].rearrange("p w j -> p (w j)"))
+                w_codes.append(wc)
+                w_scales.append(ws)
+
+        late = ctx.enter_context(tc.tile_pool(name="late", bufs=2))
+        n_sb = {}
+
+        def stage_x(i):
+            y = work.tile([P, D], F32, name="y", tag="y")
+            w = D // B_PIECES[i]
+            for k in range(B_PIECES[i]):
+                ks = slice(k * w, (k + 1) * w)
+                nc.gpsimd.tensor_tensor(out=y[:, ks], in0=r_sb[i][:, ks], in1=b_bc[:, ks], op=ALU.add)
+            a, e = divmod(i, 2)
+            for c in range(NCH):
+                acc = psum.tile([P, CH], F32, name="acc", tag="acc", bufs=2)
+                nc.tensor.matmul_mx(
+                    out=acc[:],
+                    lhsT=x_codes[a][:, e * P:(e + 1) * P].bitcast(FP8X4),
+                    lhsT_scale=x_scales[a][:, e * P:(e + 1) * P],
+                    rhs=w_codes[c][:].bitcast(FP8X4),
+                    rhs_scale=w_scales[c][:],
+                    start=True,
+                    stop=True,
+                )
+                cs = slice(c * CH, (c + 1) * CH)
+                nc.vector.scalar_tensor_tensor(
+                    out=y[:, cs], in0=acc[:], scalar=1.0, in1=y[:, cs], op0=ALU.mult, op1=ALU.add,
+                    accum_out=sums[:, i, c:c + 1],
+                )
+            nc.vector.tensor_scalar(
+                out=sums_s[:, i, :], in0=sums[:, i, :], scalar1=-1.0 / D, scalar2=None, op0=ALU.mult, op1=ALU.add,
+                accum_out=negmu[:, i:i + 1],
+            )
+            sq = late.tile([P, D], BF16, name="sq", tag="sq")
+            nc.scalar.activation(
+                out=sq[:], in_=y[:], func=ACT.Square, bias=negmu[:, i:i + 1], scale=1.0, accum_out=ssq[:, i:i + 1]
+            )
+            nc.scalar.activation(out=sd[:, i:i + 1], in_=ssq[:, i:i + 1], func=ACT.Sqrt, bias=LN_EPS, scale=1.0 / D)
+            nc.vector.reciprocal(out=rstd[:, i:i + 1], in_=sd[:, i:i + 1])
+            eng = nc.gpsimd if N_ON_GPSIMD[i] else nc.vector
+            eng.tensor_scalar(
+                out=y[:], in0=y[:], scalar1=negmu[:, i:i + 1], scalar2=rstd[:, i:i + 1], op0=ALU.add, op1=ALU.mult
+            )
+            n_sb[i] = y
+
+        def stage_y(q):
+            steps = NJ // 2
+            o_t = {}
+            t2 = {}
+            for s in range(steps + 1):
+                if s < steps:
+                    t1 = psum.tile([P, 2, NB, P], F32, name="t1", tag="t1")
+                    for jj in range(2):
+                        j = 2 * s + jj
+                        for e in range(NB):
+                            nc.tensor.transpose(t1[:, jj, e, :], n_sb[NB * q + e][:, j * P:(j + 1) * P], ident[:])
+                    ot = late.tile([P, 2, NB, P], F32, name="ot", tag="ot", bufs=4)
+                    for jj in range(2):
+                        j = 2 * s + jj
+                        nc.scalar.activation(
+                            out=ot[:, jj, :, :], in_=t1[:, jj, :, :], func=ACT.Identity,
+                            scale=gb_col[:, j:j + 1], bias=gb_col[:, NJ + j:NJ + j + 1],
+                        )
+                    o_t[s] = ot
+                if s >= 1:
+                    sp = s - 1
+                    if sp % 2 == 0:
+                        for e in range(NB):
+                            t2[e] = psum.tile([P, CH], F32, name="t2", tag="t2")
+                    for e in range(NB):
+                        for jj in range(2):
+                            j = 2 * sp + jj
+                            nc.tensor.transpose(t2[e][:, (j % 4) * P:(j % 4 + 1) * P], o_t[sp][:, jj, e, :], ident[:])
+                    if sp % 2 == 1:
+                        g4 = sp // 2
+                        for e in range(NB):
+                            i = NB * q + e
+                            dst = o_sb[i][:, g4 * CH:(g4 + 1) * CH]
+                            if CPO_ON_VECTOR[g4 * 2 + e]:
+                                nc.vector.tensor_copy(out=dst, in_=t2[e][:])
+                            else:
+                                nc.scalar.copy(out=dst, in_=t2[e][:])
+                            nc.vector.tensor_reduce(
+                                out=am[:, i * NCH + g4:i * NCH + g4 + 1], in_=dst, axis=AX.X, op=ALU.max,
+                                apply_absolute_value=True,
+                            )
+            for e in range(NB):
+                i = NB * q + e
+                nc.sync.dma_start(out=o0_view[i], in_=o_sb[i][:])
+
+        stage_x(0)
+        stage_x(1)
+
+        gbt = psum.tile([P, P], BF16, name="gbt", tag="t1")
+        nc.tensor.transpose(gbt[:], gb_rows[:], ident_b[:])
+        nc.vector.tensor_copy(out=gb_col[:], in_=gbt[:, 0:2 * NJ])
+
+        prepare_x(1)
+        for q in range(NQ):
+            if q + 1 < NQ:
+                for e in range(NB):
+                    stage_x(NB * (q + 1) + e)
+            if q + 2 < NQ:
+                prepare_x(q + 2)
+            stage_y(q)
+
+        pm = keep.tile([P, 1], F32, name="pm")
+        nc.vector.tensor_reduce(out=pm[:], in_=am[:], axis=AX.X, op=ALU.max)
+        pt = psum.tile([P, P], F32, name="pt", tag="t1")
+        nc.tensor.transpose(pt[:], pm[:, 0:1].to_broadcast([P, P]), ident[:])
+        gm = keep.tile([P, 1], F32, name="gm")
+        nc.vector.tensor_reduce(out=gm[:], in_=pt[:], axis=AX.X, op=ALU.max)
+        rc = keep.tile([P, 1], F32, name="rc")
+        nc.vector.reciprocal(out=rc[:], in_=gm[:])
+        fac = keep.tile([P, 1], F32, name="fac")
+        nc.vector.tensor_scalar(out=fac[:], in0=rc[:], scalar1=448.0, scalar2=None, op0=ALU.mult)
+
+        for i in range(NT):
+            f8 = work.tile([P, D], FP8, name="f8", tag="y")
+            o = o_sb[i]
+            nc.vector.tensor_scalar(
+                out=f8[:, 0:CAST_V], in0=o[:, 0:CAST_V], scalar1=fac[:, 0:1], scalar2=None, op0=ALU.mult,
+                saturate=False,
+            )
+            nc.scalar.activation(
+                out=f8[:, CAST_V:D], in_=o[:, CAST_V:D], func=ACT.Identity, scale=fac[:, 0:1],
+                bias=zeros[:, 0:1], saturate=False,
+            )
+            nc.sync.dma_start(out=o1_view[i], in_=f8[:].bitcast(U8))

@@ -26,19 +26,19 @@ LN_EPS = 1e-5
 FLOPS = 2 * LQ * K * D
 
 CAST_V = 1344
-NB = 2
-NQ = NT // NB
 NJ = D // P
+BATCHES = ((0,), (1, 2), (3, 4), (5, 6), (7,))
 N_ON_GPSIMD = (0, 0, 0, 0, 0, 0, 0, 0)
-CPO_ON_VECTOR = (0, 1, 0, 0, 0, 1, 0, 0)
-B_PIECES = (4, 4, 1, 1, 1, 1, 1, 1)
+CPO_ON_VECTOR = ((), (1, 5), (1, 5), (1, 3, 5), (0, 4))
+B_PIECES = 8
+R_BUFS = 4
 
 
 def tile_multiheadattention_pb_kernel(tc, attn_out, residual, proj_w, proj_b, ln_g, ln_b, out_0, out_1):
     nc = tc.nc
     with ExitStack() as ctx:
         keep = ctx.enter_context(tc.tile_pool(name="keep", bufs=1))
-        work = ctx.enter_context(tc.tile_pool(name="work", bufs=6))
+        work = ctx.enter_context(tc.tile_pool(name="work", bufs=8))
         psum = ctx.enter_context(tc.psum_pool(name="psum", bufs=3))
 
         x_view = attn_out.rearrange("h (p i) j -> i p h j", i=NT)
@@ -50,9 +50,12 @@ def tile_multiheadattention_pb_kernel(tc, attn_out, residual, proj_w, proj_b, ln
         x_sb = []
         for i in range(NT):
             x_sb.append(keep.tile([P, H, DV], BF16, name="x_sb%d" % i))
-        r_sb = []
-        for i in range(NT):
-            r_sb.append(keep.tile([P, D], BF16, name="r_sb%d" % i))
+        r_sb = {}
+
+        def load_r(i):
+            r_sb[i] = work.tile([P, D], BF16, name="r_sb", tag="r_sb", bufs=R_BUFS)
+            nc.sync.dma_start(out=r_sb[i][:], in_=r_view[i])
+
         b_bc = keep.tile([P, D], BF16, name="b_bc")
         gb_rows = keep.tile([P, P], BF16, name="gb_rows")
         o_sb = []
@@ -116,17 +119,18 @@ def tile_multiheadattention_pb_kernel(tc, attn_out, residual, proj_w, proj_b, ln
             for i in (0, 1):
                 nc.sync.dma_start(out=x_sb[i][:], in_=x_view[i])
             nc.sync.dma_start(out=b_row[0:1, :], in_=proj_b.rearrange("(o d) -> o d", o=1))
-            nc.sync.dma_start(out=r_sb[0][:], in_=r_view[0])
+            load_r(0)
             for c in range(NCH):
                 nc.sync.dma_start(out=w_raw[c][:], in_=w_view[:, :, c * CH:(c + 1) * CH])
-            nc.sync.dma_start(out=r_sb[1][:], in_=r_view[1])
+            load_r(1)
             nc.sync.dma_start(out=gb_rows[0:NJ, :], in_=ln_g.rearrange("(j p) -> j p", p=P))
             nc.sync.dma_start(out=gb_rows[NJ:2 * NJ, :], in_=ln_b.rearrange("(j p) -> j p", p=P))
             for a in range(1, NT // 2):
                 for e in range(2):
                     nc.sync.dma_start(out=x_sb[2 * a + e][:], in_=x_view[2 * a + e])
-                for e in range(2):
-                    nc.sync.dma_start(out=r_sb[2 * a + e][:], in_=r_view[2 * a + e])
+                if a == 1:
+                    load_r(2)
+                    load_r(3)
 
             prepare_x(0)
 
@@ -154,10 +158,12 @@ def tile_multiheadattention_pb_kernel(tc, attn_out, residual, proj_w, proj_b, ln
 
         def stage_x(i):
             y = work.tile([P, D], F32, name="y", tag="y")
-            w = D // B_PIECES[i]
-            for k in range(B_PIECES[i]):
+            w = D // B_PIECES
+            for k in range(B_PIECES):
                 ks = slice(k * w, (k + 1) * w)
                 nc.gpsimd.tensor_tensor(out=y[:, ks], in0=r_sb[i][:, ks], in1=b_bc[:, ks], op=ALU.add)
+            if i + R_BUFS < NT:
+                load_r(i + R_BUFS)
             a, e = divmod(i, 2)
             for c in range(NCH):
                 acc = psum.tile([P, CH], F32, name="acc", tag="acc", bufs=2)
@@ -191,20 +197,22 @@ def tile_multiheadattention_pb_kernel(tc, attn_out, residual, proj_w, proj_b, ln
             )
             n_sb[i] = y
 
-        def stage_y(q):
-            steps = NJ // 2
+        def stage_y(tiles, on_vector):
+            nb = len(tiles)
+            jn = 4 // nb
+            steps = NJ // jn
             o_t = {}
             t2 = {}
             for s in range(steps + 1):
                 if s < steps:
-                    t1 = psum.tile([P, 2, NB, P], F32, name="t1", tag="t1")
-                    for jj in range(2):
-                        j = 2 * s + jj
-                        for e in range(NB):
-                            nc.tensor.transpose(t1[:, jj, e, :], n_sb[NB * q + e][:, j * P:(j + 1) * P], ident[:])
-                    ot = late.tile([P, 2, NB, P], F32, name="ot", tag="ot", bufs=4)
-                    for jj in range(2):
-                        j = 2 * s + jj
+                    t1 = psum.tile([P, jn, nb, P], F32, name="t1", tag="t1")
+                    for jj in range(jn):
+                        j = jn * s + jj
+                        for e in range(nb):
+                            nc.tensor.transpose(t1[:, jj, e, :], n_sb[tiles[e]][:, j * P:(j + 1) * P], ident[:])
+                    ot = late.tile([P, jn, nb, P], F32, name="ot", tag="ot", bufs=4)
+                    for jj in range(jn):
+                        j = jn * s + jj
                         nc.scalar.activation(
                             out=ot[:, jj, :, :], in_=t1[:, jj, :, :], func=ACT.Identity,
                             scale=gb_col[:, j:j + 1], bias=gb_col[:, NJ + j:NJ + j + 1],
@@ -212,19 +220,19 @@ def tile_multiheadattention_pb_kernel(tc, attn_out, residual, proj_w, proj_b, ln
                     o_t[s] = ot
                 if s >= 1:
                     sp = s - 1
-                    if sp % 2 == 0:
-                        for e in range(NB):
+                    if sp % nb == 0:
+                        for e in range(nb):
                             t2[e] = psum.tile([P, CH], F32, name="t2", tag="t2")
-                    for e in range(NB):
-                        for jj in range(2):
-                            j = 2 * sp + jj
+                    for e in range(nb):
+                        for jj in range(jn):
+                            j = jn * sp + jj
                             nc.tensor.transpose(t2[e][:, (j % 4) * P:(j % 4 + 1) * P], o_t[sp][:, jj, e, :], ident[:])
-                    if sp % 2 == 1:
-                        g4 = sp // 2
-                        for e in range(NB):
-                            i = NB * q + e
+                    if sp % nb == nb - 1:
+                        g4 = sp // nb
+                        for e in range(nb):
+                            i = tiles[e]
                             dst = o_sb[i][:, g4 * CH:(g4 + 1) * CH]
-                            if CPO_ON_VECTOR[g4 * 2 + e]:
+                            if 2 * g4 + e in on_vector:
                                 nc.vector.tensor_copy(out=dst, in_=t2[e][:])
                             else:
                                 nc.scalar.copy(out=dst, in_=t2[e][:])
@@ -232,25 +240,25 @@ def tile_multiheadattention_pb_kernel(tc, attn_out, residual, proj_w, proj_b, ln
                                 out=am[:, i * NCH + g4:i * NCH + g4 + 1], in_=dst, axis=AX.X, op=ALU.max,
                                 apply_absolute_value=True,
                             )
-            for e in range(NB):
-                i = NB * q + e
+            for i in tiles:
                 nc.sync.dma_start(out=o0_view[i], in_=o_sb[i][:])
 
-        stage_x(0)
-        stage_x(1)
+        def stage_x_with_operand(i):
+            if i % 2 == 0 and i > 0:
+                prepare_x(i // 2)
+            stage_x(i)
+
+        stage_x_with_operand(0)
 
         gbt = psum.tile([P, P], BF16, name="gbt", tag="t1")
         nc.tensor.transpose(gbt[:], gb_rows[:], ident_b[:])
         nc.vector.tensor_copy(out=gb_col[:], in_=gbt[:, 0:2 * NJ])
 
-        prepare_x(1)
-        for q in range(NQ):
-            if q + 1 < NQ:
-                for e in range(NB):
-                    stage_x(NB * (q + 1) + e)
-            if q + 2 < NQ:
-                prepare_x(q + 2)
-            stage_y(q)
+        for q in range(len(BATCHES)):
+            if q + 1 < len(BATCHES):
+                for i in BATCHES[q + 1]:
+                    stage_x_with_operand(i)
+            stage_y(BATCHES[q], CPO_ON_VECTOR[q])
 
         pm = keep.tile([P, 1], F32, name="pm")
         nc.vector.tensor_reduce(out=pm[:], in_=am[:], axis=AX.X, op=ALU.max)

@@ -27,10 +27,10 @@ FLOPS = 2 * LQ * K * D
 
 CAST_V = 1344
 NJ = D // P
-BATCHES = ((0,), (1, 2), (3, 4), (5, 6), (7,))
-N_ON_GPSIMD = (0, 0, 0, 0, 0, 0, 0, 0)
-CPO_ON_VECTOR = ((), (1, 5), (1, 5), (1, 3, 5), (0, 4))
-B_PIECES = 8
+VD = 1024
+J0 = VD // P
+BATCHES = ((0, 1), (2, 3), (4, 5), (6, 7))
+B_PIECES = (4, 1, 1, 1, 1, 1, 1, 1)
 R_BUFS = 4
 
 
@@ -39,7 +39,8 @@ def tile_multiheadattention_pb_kernel(tc, attn_out, residual, proj_w, proj_b, ln
     with ExitStack() as ctx:
         keep = ctx.enter_context(tc.tile_pool(name="keep", bufs=1))
         work = ctx.enter_context(tc.tile_pool(name="work", bufs=8))
-        psum = ctx.enter_context(tc.psum_pool(name="psum", bufs=3))
+        psum = ctx.enter_context(tc.psum_pool(name="psum", bufs=2))
+        cpsum = ctx.enter_context(tc.psum_pool(name="cpsum", bufs=1))
 
         x_view = attn_out.rearrange("h (p i) j -> i p h j", i=NT)
         w_view = proj_w.rearrange("(p j) w -> p j w", j=4)
@@ -74,8 +75,11 @@ def tile_multiheadattention_pb_kernel(tc, attn_out, residual, proj_w, proj_b, ln
         ssq = keep.tile([P, NT], F32, name="ssq")
         sd = keep.tile([P, NT], F32, name="sd")
         rstd = keep.tile([P, NT], F32, name="rstd")
+        nmr = keep.tile([P, NT], F32, name="nmr")
         am = keep.tile([P, NT * NCH], F32, name="am")
         gb_col = keep.tile([P, 2 * NJ], F32, name="gb_col")
+        g_ps = cpsum.tile([P, VD], BF16, name="g_ps")
+        be_ps = cpsum.tile([P, VD], BF16, name="be_ps")
 
         x_codes = {}
         x_scales = {}
@@ -89,12 +93,10 @@ def tile_multiheadattention_pb_kernel(tc, attn_out, residual, proj_w, proj_b, ln
                 for u in range(2):
                     nc.tensor.transpose(xt[:, e, u, :], words[:, u::2], ident[:])
             xg = keep.tile([P, 2 * P * 4], BF16, name="xg%d" % a, align_bytes=64)
-            dst = xg[:].bitcast(F32).rearrange("p (e r u) -> p e r u", e=2, u=2)
-            src = xt[:].rearrange("p e u r -> p e r u")
-            if a == 0:
-                nc.vector.tensor_copy(out=dst, in_=src)
-            else:
-                nc.scalar.copy(out=dst, in_=src)
+            nc.scalar.copy(
+                out=xg[:].bitcast(F32).rearrange("p (e r u) -> p e r u", e=2, u=2),
+                in_=xt[:].rearrange("p e u r -> p e r u"),
+            )
             xc = keep.tile([P, 2 * P], U32, name="x_codes%d" % a, align_bytes=64)
             xs = keep.tile([P, 2 * P], U8, name="x_scales%d" % a, align_bytes=64)
             nc.vector.quantize_mx(out=xc[:].bitcast(FP8X4), scales=xs[:], in_=xg[:])
@@ -105,9 +107,9 @@ def tile_multiheadattention_pb_kernel(tc, attn_out, residual, proj_w, proj_b, ln
             w_raw = []
             for c in range(NCH):
                 w_raw.append(wpool.tile([P, 4, CH], BF16, name="w_raw%d" % c))
-            b_row = wpool.tile([P, D], BF16, name="b_row")
+            rows = wpool.tile([P, D + 2 * VD], BF16, name="rows")
 
-            nc.vector.memset(b_row[:], 0.0)
+            nc.vector.memset(rows[:], 0.0)
             nc.vector.memset(ones_b[:], 1.0)
             nc.vector.memset(gb_rows[:], 0.0)
             nc.vector.memset(ones[:], 1.0)
@@ -118,11 +120,13 @@ def tile_multiheadattention_pb_kernel(tc, attn_out, residual, proj_w, proj_b, ln
 
             for i in (0, 1):
                 nc.sync.dma_start(out=x_sb[i][:], in_=x_view[i])
-            nc.sync.dma_start(out=b_row[0:1, :], in_=proj_b.rearrange("(o d) -> o d", o=1))
+            nc.sync.dma_start(out=rows[0:1, 0:D], in_=proj_b.rearrange("(o d) -> o d", o=1))
             load_r(0)
             for c in range(NCH):
                 nc.sync.dma_start(out=w_raw[c][:], in_=w_view[:, :, c * CH:(c + 1) * CH])
             load_r(1)
+            nc.sync.dma_start(out=rows[0:1, D:D + VD], in_=ln_g.rearrange("(o d) -> o d", o=1)[:, 0:VD])
+            nc.sync.dma_start(out=rows[0:1, D + VD:D + 2 * VD], in_=ln_b.rearrange("(o d) -> o d", o=1)[:, 0:VD])
             nc.sync.dma_start(out=gb_rows[0:NJ, :], in_=ln_g.rearrange("(j p) -> j p", p=P))
             nc.sync.dma_start(out=gb_rows[NJ:2 * NJ, :], in_=ln_b.rearrange("(j p) -> j p", p=P))
             for a in range(1, NT // 2):
@@ -137,7 +141,7 @@ def tile_multiheadattention_pb_kernel(tc, attn_out, residual, proj_w, proj_b, ln
             for c in range(NCH):
                 cs = slice(c * CH, (c + 1) * CH)
                 pb = psum.tile([P, CH], F32, name="pb", tag="t1")
-                nc.tensor.matmul(out=pb[:], lhsT=ones_b[:], rhs=b_row[:, cs], start=True, stop=True)
+                nc.tensor.matmul(out=pb[:], lhsT=ones_b[:], rhs=rows[:, cs], start=True, stop=True)
                 nc.scalar.copy(out=b_bc[:, cs], in_=pb[:])
 
             for c in range(NCH):
@@ -153,20 +157,32 @@ def tile_multiheadattention_pb_kernel(tc, attn_out, residual, proj_w, proj_b, ln
                 w_codes.append(wc)
                 w_scales.append(ws)
 
+            for c in range(VD // CH):
+                cs = slice(c * CH, (c + 1) * CH)
+                nc.tensor.matmul(
+                    out=g_ps[:, cs], lhsT=ones_b[:], rhs=rows[:, D + c * CH:D + (c + 1) * CH], start=True, stop=True
+                )
+                nc.tensor.matmul(
+                    out=be_ps[:, cs], lhsT=ones_b[:], rhs=rows[:, D + VD + c * CH:D + VD + (c + 1) * CH],
+                    start=True, stop=True,
+                )
+
         late = ctx.enter_context(tc.tile_pool(name="late", bufs=2))
         n_sb = {}
 
         def stage_x(i):
+            if i % 2 == 0 and i > 0:
+                prepare_x(i // 2)
             y = work.tile([P, D], F32, name="y", tag="y")
-            w = D // B_PIECES
-            for k in range(B_PIECES):
+            w = D // B_PIECES[i]
+            for k in range(B_PIECES[i]):
                 ks = slice(k * w, (k + 1) * w)
                 nc.gpsimd.tensor_tensor(out=y[:, ks], in0=r_sb[i][:, ks], in1=b_bc[:, ks], op=ALU.add)
             if i + R_BUFS < NT:
                 load_r(i + R_BUFS)
             a, e = divmod(i, 2)
             for c in range(NCH):
-                acc = psum.tile([P, CH], F32, name="acc", tag="acc", bufs=2)
+                acc = psum.tile([P, CH], F32, name="acc", tag="acc")
                 nc.tensor.matmul_mx(
                     out=acc[:],
                     lhsT=x_codes[a][:, e * P:(e + 1) * P].bitcast(FP8X4),
@@ -185,34 +201,46 @@ def tile_multiheadattention_pb_kernel(tc, attn_out, residual, proj_w, proj_b, ln
                 out=sums_s[:, i, :], in0=sums[:, i, :], scalar1=-1.0 / D, scalar2=None, op0=ALU.mult, op1=ALU.add,
                 accum_out=negmu[:, i:i + 1],
             )
+            ic = slice(i, i + 1)
             sq = late.tile([P, D], BF16, name="sq", tag="sq")
+            nc.scalar.activation(out=sq[:], in_=y[:], func=ACT.Square, bias=negmu[:, ic], scale=1.0, accum_out=ssq[:, ic])
+            nc.scalar.activation(out=sd[:, ic], in_=ssq[:, ic], func=ACT.Sqrt, bias=LN_EPS, scale=1.0 / D)
+            nc.vector.reciprocal(out=rstd[:, ic], in_=sd[:, ic])
+            nc.scalar.activation(out=nmr[:, ic], in_=negmu[:, ic], func=ACT.Copy, scale=rstd[:, ic])
             nc.scalar.activation(
-                out=sq[:], in_=y[:], func=ACT.Square, bias=negmu[:, i:i + 1], scale=1.0, accum_out=ssq[:, i:i + 1]
+                out=y[:, VD:D], in_=y[:, VD:D], func=ACT.Identity, scale=rstd[:, ic], bias=nmr[:, ic]
             )
-            nc.scalar.activation(out=sd[:, i:i + 1], in_=ssq[:, i:i + 1], func=ACT.Sqrt, bias=LN_EPS, scale=1.0 / D)
-            nc.vector.reciprocal(out=rstd[:, i:i + 1], in_=sd[:, i:i + 1])
-            eng = nc.gpsimd if N_ON_GPSIMD[i] else nc.vector
-            eng.tensor_scalar(
-                out=y[:], in0=y[:], scalar1=negmu[:, i:i + 1], scalar2=rstd[:, i:i + 1], op0=ALU.add, op1=ALU.mult
+            for c in range(VD // CH):
+                cs = slice(c * CH, (c + 1) * CH)
+                nc.vector.scalar_tensor_tensor(
+                    out=y[:, cs], in0=y[:, cs], scalar=negmu[:, ic], in1=g_ps[:, cs], op0=ALU.add, op1=ALU.mult
+                )
+            for c in range(VD // CH):
+                cs = slice(c * CH, (c + 1) * CH)
+                nc.vector.scalar_tensor_tensor(
+                    out=o_sb[i][:, cs], in0=y[:, cs], scalar=rstd[:, ic], in1=be_ps[:, cs], op0=ALU.mult, op1=ALU.add
+                )
+            nc.vector.tensor_reduce(
+                out=am[:, i * NCH:i * NCH + 1], in_=o_sb[i][:, 0:VD], axis=AX.X, op=ALU.max, apply_absolute_value=True
             )
             n_sb[i] = y
 
-        def stage_y(tiles, on_vector):
+        def stage_y(tiles):
             nb = len(tiles)
             jn = 4 // nb
-            steps = NJ // jn
+            steps = (NJ - J0) // jn
             o_t = {}
             t2 = {}
             for s in range(steps + 1):
                 if s < steps:
                     t1 = psum.tile([P, jn, nb, P], F32, name="t1", tag="t1")
                     for jj in range(jn):
-                        j = jn * s + jj
+                        j = J0 + jn * s + jj
                         for e in range(nb):
                             nc.tensor.transpose(t1[:, jj, e, :], n_sb[tiles[e]][:, j * P:(j + 1) * P], ident[:])
                     ot = late.tile([P, jn, nb, P], F32, name="ot", tag="ot", bufs=4)
                     for jj in range(jn):
-                        j = jn * s + jj
+                        j = J0 + jn * s + jj
                         nc.scalar.activation(
                             out=ot[:, jj, :, :], in_=t1[:, jj, :, :], func=ACT.Identity,
                             scale=gb_col[:, j:j + 1], bias=gb_col[:, NJ + j:NJ + j + 1],
@@ -228,14 +256,11 @@ def tile_multiheadattention_pb_kernel(tc, attn_out, residual, proj_w, proj_b, ln
                             j = jn * sp + jj
                             nc.tensor.transpose(t2[e][:, (j % 4) * P:(j % 4 + 1) * P], o_t[sp][:, jj, e, :], ident[:])
                     if sp % nb == nb - 1:
-                        g4 = sp // nb
+                        g4 = VD // CH + sp // nb
                         for e in range(nb):
                             i = tiles[e]
                             dst = o_sb[i][:, g4 * CH:(g4 + 1) * CH]
-                            if 2 * g4 + e in on_vector:
-                                nc.vector.tensor_copy(out=dst, in_=t2[e][:])
-                            else:
-                                nc.scalar.copy(out=dst, in_=t2[e][:])
+                            nc.scalar.copy(out=dst, in_=t2[e][:])
                             nc.vector.tensor_reduce(
                                 out=am[:, i * NCH + g4:i * NCH + g4 + 1], in_=dst, axis=AX.X, op=ALU.max,
                                 apply_absolute_value=True,
@@ -243,12 +268,9 @@ def tile_multiheadattention_pb_kernel(tc, attn_out, residual, proj_w, proj_b, ln
             for i in tiles:
                 nc.sync.dma_start(out=o0_view[i], in_=o_sb[i][:])
 
-        def stage_x_with_operand(i):
-            if i % 2 == 0 and i > 0:
-                prepare_x(i // 2)
+        nc.vector.memset(am[:], 0.0)
+        for i in BATCHES[0]:
             stage_x(i)
-
-        stage_x_with_operand(0)
 
         gbt = psum.tile([P, P], BF16, name="gbt", tag="t1")
         nc.tensor.transpose(gbt[:], gb_rows[:], ident_b[:])
@@ -257,8 +279,8 @@ def tile_multiheadattention_pb_kernel(tc, attn_out, residual, proj_w, proj_b, ln
         for q in range(len(BATCHES)):
             if q + 1 < len(BATCHES):
                 for i in BATCHES[q + 1]:
-                    stage_x_with_operand(i)
-            stage_y(BATCHES[q], CPO_ON_VECTOR[q])
+                    stage_x(i)
+            stage_y(BATCHES[q])
 
         pm = keep.tile([P, 1], F32, name="pm")
         nc.vector.tensor_reduce(out=pm[:], in_=am[:], axis=AX.X, op=ALU.max)

@@ -28,15 +28,14 @@ FLOPS = 2 * LQ * K * D
 CAST_V = 1344
 NJ = D // P
 VD = 1024
-J0 = VD // P
-BATCHES = ((0, 1), (2, 3), (4, 5), (6, 7))
-B_PIECES = (4, 1, 1, 1, 1, 1, 1, 1)
+NU = (D - VD) // CH
 R_BUFS = 4
 
 
 def tile_multiheadattention_pb_kernel(tc, attn_out, residual, proj_w, proj_b, ln_g, ln_b, out_0, out_1):
     nc = tc.nc
     with ExitStack() as ctx:
+        ctx.enter_context(tc.manual_schedule())
         keep = ctx.enter_context(tc.tile_pool(name="keep", bufs=1))
         work = ctx.enter_context(tc.tile_pool(name="work", bufs=8))
         psum = ctx.enter_context(tc.psum_pool(name="psum", bufs=2))
@@ -51,18 +50,11 @@ def tile_multiheadattention_pb_kernel(tc, attn_out, residual, proj_w, proj_b, ln
         x_sb = []
         for i in range(NT):
             x_sb.append(keep.tile([P, H, DV], BF16, name="x_sb%d" % i))
-        r_sb = {}
-
-        def load_r(i):
-            r_sb[i] = work.tile([P, D], BF16, name="r_sb", tag="r_sb", bufs=R_BUFS)
-            nc.sync.dma_start(out=r_sb[i][:], in_=r_view[i])
-
         b_bc = keep.tile([P, D], BF16, name="b_bc")
         gb_rows = keep.tile([P, P], BF16, name="gb_rows")
         o_sb = []
         for i in range(NT):
             o_sb.append(keep.tile([P, D], F32, name="o_sb%d" % i))
-
         ident = keep.tile([P, P], F32, name="ident")
         ident_b = keep.tile([P, P], BF16, name="ident_b")
         ones_b = keep.tile([P, P], BF16, name="ones_b")
@@ -78,115 +70,64 @@ def tile_multiheadattention_pb_kernel(tc, attn_out, residual, proj_w, proj_b, ln
         nmr = keep.tile([P, NT], F32, name="nmr")
         am = keep.tile([P, NT * NCH], F32, name="am")
         gb_col = keep.tile([P, 2 * NJ], F32, name="gb_col")
+        xg = keep.tile([P, NT * P * 4], BF16, name="xg", align_bytes=64)
+        x_codes = keep.tile([P, NT * P], U32, name="x_codes", align_bytes=64)
+        x_scales = keep.tile([P, NT * P], U8, name="x_scales", align_bytes=64)
         g_ps = cpsum.tile([P, VD], BF16, name="g_ps")
         be_ps = cpsum.tile([P, VD], BF16, name="be_ps")
 
-        x_codes = {}
-        x_scales = {}
+        r_sb = {}
+        y_sb = {}
+        xt_ps = {}
+        t1_ps = {}
+        t2_ps = {}
+        ot_sb = {}
         w_codes = []
         w_scales = []
 
-        def prepare_x(a):
-            xt = psum.tile([P, 2, 2, P], F32, name="xt", tag="t2")
+        def load_x(i):
+            nc.sync.dma_start(out=x_sb[i][:], in_=x_view[i])
+
+        def load_r(i):
+            r_sb[i] = work.tile([P, D], BF16, name="r_sb", tag="r_sb", bufs=R_BUFS)
+            nc.sync.dma_start(out=r_sb[i][:], in_=r_view[i])
+
+        def x_transpose(a):
+            xt = psum.tile([P, 2, 2, P], F32, name="xt", tag="mm", bufs=4)
             for e in range(2):
                 words = x_sb[2 * a + e][:].rearrange("p h j -> p (h j)").bitcast(F32)
                 for u in range(2):
                     nc.tensor.transpose(xt[:, e, u, :], words[:, u::2], ident[:])
-            xg = keep.tile([P, 2 * P * 4], BF16, name="xg%d" % a, align_bytes=64)
+            xt_ps[a] = xt
+
+        def x_copy(a):
             nc.scalar.copy(
-                out=xg[:].bitcast(F32).rearrange("p (e r u) -> p e r u", e=2, u=2),
-                in_=xt[:].rearrange("p e u r -> p e r u"),
+                out=xg[:, a * 1024:(a + 1) * 1024].bitcast(F32).rearrange("p (e r u) -> p e r u", e=2, u=2),
+                in_=xt_ps[a][:].rearrange("p e u r -> p e r u"),
             )
-            xc = keep.tile([P, 2 * P], U32, name="x_codes%d" % a, align_bytes=64)
-            xs = keep.tile([P, 2 * P], U8, name="x_scales%d" % a, align_bytes=64)
-            nc.vector.quantize_mx(out=xc[:].bitcast(FP8X4), scales=xs[:], in_=xg[:])
-            x_codes[a] = xc
-            x_scales[a] = xs
 
-        with tc.tile_pool(name="wpool", bufs=1) as wpool:
-            w_raw = []
-            for c in range(NCH):
-                w_raw.append(wpool.tile([P, 4, CH], BF16, name="w_raw%d" % c))
-            rows = wpool.tile([P, D + 2 * VD], BF16, name="rows")
+        def x_quantise(a, n):
+            nc.vector.quantize_mx(
+                out=x_codes[:, a * 256:(a + n) * 256].bitcast(FP8X4),
+                scales=x_scales[:, a * 256:(a + n) * 256],
+                in_=xg[:, a * 1024:(a + n) * 1024],
+            )
 
-            nc.vector.memset(rows[:], 0.0)
-            nc.vector.memset(ones_b[:], 1.0)
-            nc.vector.memset(gb_rows[:], 0.0)
-            nc.vector.memset(ones[:], 1.0)
-            nc.vector.memset(zeros[:], 0.0)
-            make_identity(nc, ident[:])
-            make_identity(nc, ident_b[:])
-            nc.scalar.activation(out=warm[:], in_=ones[:], func=ACT.Sqrt)
-
-            for i in (0, 1):
-                nc.sync.dma_start(out=x_sb[i][:], in_=x_view[i])
-            nc.sync.dma_start(out=rows[0:1, 0:D], in_=proj_b.rearrange("(o d) -> o d", o=1))
-            load_r(0)
-            for c in range(NCH):
-                nc.sync.dma_start(out=w_raw[c][:], in_=w_view[:, :, c * CH:(c + 1) * CH])
-            load_r(1)
-            nc.sync.dma_start(out=rows[0:1, D:D + VD], in_=ln_g.rearrange("(o d) -> o d", o=1)[:, 0:VD])
-            nc.sync.dma_start(out=rows[0:1, D + VD:D + 2 * VD], in_=ln_b.rearrange("(o d) -> o d", o=1)[:, 0:VD])
-            nc.sync.dma_start(out=gb_rows[0:NJ, :], in_=ln_g.rearrange("(j p) -> j p", p=P))
-            nc.sync.dma_start(out=gb_rows[NJ:2 * NJ, :], in_=ln_b.rearrange("(j p) -> j p", p=P))
-            for a in range(1, NT // 2):
-                for e in range(2):
-                    nc.sync.dma_start(out=x_sb[2 * a + e][:], in_=x_view[2 * a + e])
-                if a == 1:
-                    load_r(2)
-                    load_r(3)
-
-            prepare_x(0)
-
-            for c in range(NCH):
-                cs = slice(c * CH, (c + 1) * CH)
-                pb = psum.tile([P, CH], F32, name="pb", tag="t1")
-                nc.tensor.matmul(out=pb[:], lhsT=ones_b[:], rhs=rows[:, cs], start=True, stop=True)
-                nc.scalar.copy(out=b_bc[:, cs], in_=pb[:])
-
-            for c in range(NCH):
-                wg = wpool.tile([P, CH, 4], BF16, name="wg%d" % c, align_bytes=64)
-                src = w_raw[c][:].rearrange("p j w -> p w j")
-                if c in (1, 2):
-                    nc.scalar.copy(out=wg[:], in_=src)
-                else:
-                    nc.vector.tensor_copy(out=wg[:], in_=src)
-                wc = keep.tile([P, CH], U32, name="w_codes%d" % c, align_bytes=64)
-                ws = keep.tile([P, CH], U8, name="w_scales%d" % c, align_bytes=64)
-                nc.vector.quantize_mx(out=wc[:].bitcast(FP8X4), scales=ws[:], in_=wg[:].rearrange("p w j -> p (w j)"))
-                w_codes.append(wc)
-                w_scales.append(ws)
-
-            for c in range(VD // CH):
-                cs = slice(c * CH, (c + 1) * CH)
-                nc.tensor.matmul(
-                    out=g_ps[:, cs], lhsT=ones_b[:], rhs=rows[:, D + c * CH:D + (c + 1) * CH], start=True, stop=True
-                )
-                nc.tensor.matmul(
-                    out=be_ps[:, cs], lhsT=ones_b[:], rhs=rows[:, D + VD + c * CH:D + VD + (c + 1) * CH],
-                    start=True, stop=True,
-                )
-
-        late = ctx.enter_context(tc.tile_pool(name="late", bufs=2))
-        n_sb = {}
-
-        def stage_x(i):
-            if i % 2 == 0 and i > 0:
-                prepare_x(i // 2)
-            y = work.tile([P, D], F32, name="y", tag="y")
-            w = D // B_PIECES[i]
-            for k in range(B_PIECES[i]):
+        def add_bias(i, pieces):
+            y_sb[i] = work.tile([P, D], F32, name="y", tag="y")
+            w = D // pieces
+            for k in range(pieces):
                 ks = slice(k * w, (k + 1) * w)
-                nc.gpsimd.tensor_tensor(out=y[:, ks], in0=r_sb[i][:, ks], in1=b_bc[:, ks], op=ALU.add)
-            if i + R_BUFS < NT:
-                load_r(i + R_BUFS)
-            a, e = divmod(i, 2)
+                nc.gpsimd.tensor_tensor(out=y_sb[i][:, ks], in0=r_sb[i][:, ks], in1=b_bc[:, ks], op=ALU.add)
+
+        def project(i):
+            y = y_sb[i]
             for c in range(NCH):
-                acc = psum.tile([P, CH], F32, name="acc", tag="acc")
+                acc = psum.tile([P, CH], F32, name="acc", tag="mm", bufs=4)
                 nc.tensor.matmul_mx(
                     out=acc[:],
-                    lhsT=x_codes[a][:, e * P:(e + 1) * P].bitcast(FP8X4),
-                    lhsT_scale=x_scales[a][:, e * P:(e + 1) * P],
+                    lhsT=x_codes[:, i * P:(i + 1) * P].bitcast(FP8X4),
+                    lhsT_scale=x_scales[:, i * P:(i + 1) * P],
                     rhs=w_codes[c][:].bitcast(FP8X4),
                     rhs_scale=w_scales[c][:],
                     start=True,
@@ -201,15 +142,26 @@ def tile_multiheadattention_pb_kernel(tc, attn_out, residual, proj_w, proj_b, ln
                 out=sums_s[:, i, :], in0=sums[:, i, :], scalar1=-1.0 / D, scalar2=None, op0=ALU.mult, op1=ALU.add,
                 accum_out=negmu[:, i:i + 1],
             )
+
+        def variance(i):
             ic = slice(i, i + 1)
             sq = late.tile([P, D], BF16, name="sq", tag="sq")
-            nc.scalar.activation(out=sq[:], in_=y[:], func=ACT.Square, bias=negmu[:, ic], scale=1.0, accum_out=ssq[:, ic])
+            nc.scalar.activation(
+                out=sq[:], in_=y_sb[i][:], func=ACT.Square, bias=negmu[:, ic], scale=1.0, accum_out=ssq[:, ic]
+            )
             nc.scalar.activation(out=sd[:, ic], in_=ssq[:, ic], func=ACT.Sqrt, bias=LN_EPS, scale=1.0 / D)
+
+        def normalise(i):
+            ic = slice(i, i + 1)
             nc.vector.reciprocal(out=rstd[:, ic], in_=sd[:, ic])
             nc.scalar.activation(out=nmr[:, ic], in_=negmu[:, ic], func=ACT.Copy, scale=rstd[:, ic])
             nc.scalar.activation(
-                out=y[:, VD:D], in_=y[:, VD:D], func=ACT.Identity, scale=rstd[:, ic], bias=nmr[:, ic]
+                out=y_sb[i][:, VD:D], in_=y_sb[i][:, VD:D], func=ACT.Identity, scale=rstd[:, ic], bias=nmr[:, ic]
             )
+
+        def direct(i):
+            ic = slice(i, i + 1)
+            y = y_sb[i]
             for c in range(VD // CH):
                 cs = slice(c * CH, (c + 1) * CH)
                 nc.vector.scalar_tensor_tensor(
@@ -223,64 +175,192 @@ def tile_multiheadattention_pb_kernel(tc, attn_out, residual, proj_w, proj_b, ln
             nc.vector.tensor_reduce(
                 out=am[:, i * NCH:i * NCH + 1], in_=o_sb[i][:, 0:VD], axis=AX.X, op=ALU.max, apply_absolute_value=True
             )
-            n_sb[i] = y
 
-        def stage_y(tiles):
-            nb = len(tiles)
-            jn = 4 // nb
-            steps = (NJ - J0) // jn
-            o_t = {}
-            t2 = {}
-            for s in range(steps + 1):
-                if s < steps:
-                    t1 = psum.tile([P, jn, nb, P], F32, name="t1", tag="t1")
-                    for jj in range(jn):
-                        j = J0 + jn * s + jj
-                        for e in range(nb):
-                            nc.tensor.transpose(t1[:, jj, e, :], n_sb[tiles[e]][:, j * P:(j + 1) * P], ident[:])
-                    ot = late.tile([P, jn, nb, P], F32, name="ot", tag="ot", bufs=4)
-                    for jj in range(jn):
-                        j = J0 + jn * s + jj
-                        nc.scalar.activation(
-                            out=ot[:, jj, :, :], in_=t1[:, jj, :, :], func=ACT.Identity,
-                            scale=gb_col[:, j:j + 1], bias=gb_col[:, NJ + j:NJ + j + 1],
-                        )
-                    o_t[s] = ot
-                if s >= 1:
-                    sp = s - 1
-                    if sp % nb == 0:
-                        for e in range(nb):
-                            t2[e] = psum.tile([P, CH], F32, name="t2", tag="t2")
-                    for e in range(nb):
-                        for jj in range(jn):
-                            j = jn * sp + jj
-                            nc.tensor.transpose(t2[e][:, (j % 4) * P:(j % 4 + 1) * P], o_t[sp][:, jj, e, :], ident[:])
-                    if sp % nb == nb - 1:
-                        g4 = VD // CH + sp // nb
-                        for e in range(nb):
-                            i = tiles[e]
-                            dst = o_sb[i][:, g4 * CH:(g4 + 1) * CH]
-                            nc.scalar.copy(out=dst, in_=t2[e][:])
-                            nc.vector.tensor_reduce(
-                                out=am[:, i * NCH + g4:i * NCH + g4 + 1], in_=dst, axis=AX.X, op=ALU.max,
-                                apply_absolute_value=True,
-                            )
-            for i in tiles:
-                nc.sync.dma_start(out=o0_view[i], in_=o_sb[i][:])
+        def to_features(u):
+            q, h = divmod(u, NU)
+            t1_ps[u] = []
+            for s in range(2):
+                t1 = psum.tile([P, 2, 2, P], F32, name="t1", tag="t1")
+                for jj in range(2):
+                    c0 = VD + h * CH + (2 * s + jj) * P
+                    for e in range(2):
+                        nc.tensor.transpose(t1[:, jj, e, :], y_sb[2 * q + e][:, c0:c0 + P], ident[:])
+                t1_ps[u].append(t1)
 
-        nc.vector.memset(am[:], 0.0)
-        for i in BATCHES[0]:
-            stage_x(i)
+        def gain_bias(u):
+            q, h = divmod(u, NU)
+            ot_sb[u] = []
+            for s in range(2):
+                ot = late.tile([P, 2, 2, P], F32, name="ot", tag="ot", bufs=4)
+                for jj in range(2):
+                    j = (VD + h * CH) // P + 2 * s + jj
+                    nc.scalar.activation(
+                        out=ot[:, jj, :, :], in_=t1_ps[u][s][:, jj, :, :], func=ACT.Identity,
+                        scale=gb_col[:, j:j + 1], bias=gb_col[:, NJ + j:NJ + j + 1],
+                    )
+                ot_sb[u].append(ot)
+
+        def to_tokens(u):
+            t2_ps[u] = []
+            for e in range(2):
+                t2_ps[u].append(psum.tile([P, CH], F32, name="t2", tag="mm", bufs=4))
+            for s in range(2):
+                for e in range(2):
+                    for jj in range(2):
+                        k = 2 * s + jj
+                        nc.tensor.transpose(t2_ps[u][e][:, k * P:(k + 1) * P], ot_sb[u][s][:, jj, e, :], ident[:])
+
+        def copy_out(u):
+            q, h = divmod(u, NU)
+            for e in range(2):
+                c0 = VD + h * CH
+                nc.scalar.copy(out=o_sb[2 * q + e][:, c0:c0 + CH], in_=t2_ps[u][e][:])
+
+        def unit_absmax(u):
+            q, h = divmod(u, NU)
+            for e in range(2):
+                i = 2 * q + e
+                c0 = VD + h * CH
+                k = i * NCH + VD // CH + h
+                nc.vector.tensor_reduce(
+                    out=am[:, k:k + 1], in_=o_sb[i][:, c0:c0 + CH], axis=AX.X, op=ALU.max, apply_absolute_value=True
+                )
+            if h == NU - 1:
+                for e in range(2):
+                    nc.sync.dma_start(out=o0_view[2 * q + e], in_=o_sb[2 * q + e][:])
+
+        with tc.tile_pool(name="wpool", bufs=1) as wpool:
+            w_raw = []
+            wg = []
+            for c in range(NCH):
+                w_raw.append(wpool.tile([P, 4, CH], BF16, name="w_raw%d" % c))
+                wg.append(wpool.tile([P, CH, 4], BF16, name="wg%d" % c, align_bytes=64))
+                w_codes.append(keep.tile([P, CH], U32, name="w_codes%d" % c, align_bytes=64))
+                w_scales.append(keep.tile([P, CH], U8, name="w_scales%d" % c, align_bytes=64))
+            rows = wpool.tile([P, D + 2 * VD], BF16, name="rows")
+
+            def load_w(c):
+                nc.sync.dma_start(out=w_raw[c][:], in_=w_view[:, :, c * CH:(c + 1) * CH])
+
+            def w_interleave(c, eng):
+                src = w_raw[c][:].rearrange("p j w -> p w j")
+                if eng == "scalar":
+                    nc.scalar.copy(out=wg[c][:], in_=src)
+                else:
+                    nc.vector.tensor_copy(out=wg[c][:], in_=src)
+
+            def w_quantise(c):
+                nc.vector.quantize_mx(
+                    out=w_codes[c][:].bitcast(FP8X4), scales=w_scales[c][:], in_=wg[c][:].rearrange("p w j -> p (w j)")
+                )
+
+            nc.vector.memset(rows[:], 0.0)
+            nc.vector.memset(ones_b[:], 1.0)
+            nc.vector.memset(gb_rows[:], 0.0)
+            nc.vector.memset(ones[:], 1.0)
+            nc.vector.memset(zeros[:], 0.0)
+            nc.vector.memset(am[:], 0.0)
+            make_identity(nc, ident[:])
+            make_identity(nc, ident_b[:])
+            nc.scalar.activation(out=warm[:], in_=ones[:], func=ACT.Sqrt)
+
+            load_x(0)
+            load_x(1)
+            load_r(0)
+            load_w(0)
+            nc.sync.dma_start(out=rows[0:1, 0:D], in_=proj_b.rearrange("(o d) -> o d", o=1))
+            nc.sync.dma_start(out=rows[0:1, D:D + VD], in_=ln_g.rearrange("(o d) -> o d", o=1)[:, 0:VD])
+            nc.sync.dma_start(out=rows[0:1, D + VD:D + 2 * VD], in_=ln_b.rearrange("(o d) -> o d", o=1)[:, 0:VD])
+            nc.sync.dma_start(out=gb_rows[0:NJ, :], in_=ln_g.rearrange("(j p) -> j p", p=P))
+            nc.sync.dma_start(out=gb_rows[NJ:2 * NJ, :], in_=ln_b.rearrange("(j p) -> j p", p=P))
+            for c in range(1, NCH):
+                load_w(c)
+            for i in range(2, NT):
+                load_x(i)
+            load_r(1)
+            load_r(2)
+            load_r(3)
+
+            x_transpose(0)
+            x_copy(0)
+            x_quantise(0, 1)
+
+            for c in range(NCH):
+                cs = slice(c * CH, (c + 1) * CH)
+                pb = psum.tile([P, CH], F32, name="pb", tag="t1")
+                nc.tensor.matmul(out=pb[:], lhsT=ones_b[:], rhs=rows[:, cs], start=True, stop=True)
+                nc.scalar.copy(out=b_bc[:, cs], in_=pb[:])
+            add_bias(0, 4)
+
+            w_interleave(0, "vector")
+            w_quantise(0)
+            w_interleave(1, "scalar")
+            w_interleave(2, "vector")
+            w_quantise(2)
+            w_interleave(3, "scalar")
+            w_quantise(1)
+            w_quantise(3)
+
+            for c in range(VD // CH):
+                cs = slice(c * CH, (c + 1) * CH)
+                nc.tensor.matmul(
+                    out=g_ps[:, cs], lhsT=ones_b[:], rhs=rows[:, D + c * CH:D + (c + 1) * CH], start=True, stop=True
+                )
+                nc.tensor.matmul(
+                    out=be_ps[:, cs], lhsT=ones_b[:], rhs=rows[:, D + VD + c * CH:D + VD + (c + 1) * CH],
+                    start=True, stop=True,
+                )
+
+        late = ctx.enter_context(tc.tile_pool(name="late", bufs=2))
 
         gbt = psum.tile([P, P], BF16, name="gbt", tag="t1")
         nc.tensor.transpose(gbt[:], gb_rows[:], ident_b[:])
         nc.vector.tensor_copy(out=gb_col[:], in_=gbt[:, 0:2 * NJ])
 
-        for q in range(len(BATCHES)):
-            if q + 1 < len(BATCHES):
-                for i in BATCHES[q + 1]:
-                    stage_x(i)
-            stage_y(BATCHES[q])
+        add_bias(1, 4)
+        load_r(4)
+        load_r(5)
+        for a in range(1, NT // 2):
+            x_transpose(a)
+            x_copy(a)
+        project(0)
+        variance(0)
+        x_quantise(1, 1)
+        x_quantise(2, 2)
+        add_bias(2, 1)
+        load_r(6)
+        project(1)
+        variance(1)
+        add_bias(3, 1)
+        load_r(7)
+        normalise(0)
+
+        for t in range(NT):
+            if 0 < t < NT - 1:
+                normalise(t + 1)
+            if t + 4 < NT:
+                add_bias(t + 4, 1)
+            if t + 2 < NT:
+                project(t + 2)
+            if t == 0:
+                normalise(1)
+            if t >= 1:
+                gain_bias(t - 1)
+            if t + 2 < NT:
+                variance(t + 2)
+            if t >= 1:
+                to_tokens(t - 1)
+            to_features(t)
+            direct(t)
+            if t >= 1:
+                copy_out(t - 1)
+            if t >= 2:
+                unit_absmax(t - 2)
+        gain_bias(NT - 1)
+        to_tokens(NT - 1)
+        unit_absmax(NT - 2)
+        copy_out(NT - 1)
+        unit_absmax(NT - 1)
 
         pm = keep.tile([P, 1], F32, name="pm")
         nc.vector.tensor_reduce(out=pm[:], in_=am[:], axis=AX.X, op=ALU.max)

@@ -113,12 +113,16 @@ def tile_multiheadattention_pb_kernel(tc, attn_out, residual, proj_w, proj_b, ln
                 in_=xg[:, a * 1024:(a + n) * 1024],
             )
 
-        def add_bias(i, pieces):
-            y_sb[i] = work.tile([P, D], F32, name="y", tag="y")
+        def add_bias_piece(i, k, pieces):
+            if k == 0:
+                y_sb[i] = work.tile([P, D], F32, name="y", tag="y")
             w = D // pieces
+            ks = slice(k * w, (k + 1) * w)
+            nc.gpsimd.tensor_tensor(out=y_sb[i][:, ks], in0=r_sb[i][:, ks], in1=b_bc[:, ks], op=ALU.add)
+
+        def add_bias(i, pieces):
             for k in range(pieces):
-                ks = slice(k * w, (k + 1) * w)
-                nc.gpsimd.tensor_tensor(out=y_sb[i][:, ks], in0=r_sb[i][:, ks], in1=b_bc[:, ks], op=ALU.add)
+                add_bias_piece(i, k, pieces)
 
         def project(i):
             y = y_sb[i]
@@ -138,13 +142,12 @@ def tile_multiheadattention_pb_kernel(tc, attn_out, residual, proj_w, proj_b, ln
                     out=y[:, cs], in0=acc[:], scalar=1.0, in1=y[:, cs], op0=ALU.mult, op1=ALU.add,
                     accum_out=sums[:, i, c:c + 1],
                 )
-            nc.vector.tensor_scalar(
-                out=sums_s[:, i, :], in0=sums[:, i, :], scalar1=-1.0 / D, scalar2=None, op0=ALU.mult, op1=ALU.add,
-                accum_out=negmu[:, i:i + 1],
-            )
 
         def variance(i):
             ic = slice(i, i + 1)
+            nc.scalar.activation(
+                out=sums_s[:, i, :], in_=sums[:, i, :], func=ACT.Copy, scale=-1.0 / D, accum_out=negmu[:, ic]
+            )
             sq = late.tile([P, D], BF16, name="sq", tag="sq")
             nc.scalar.activation(
                 out=sq[:], in_=y_sb[i][:], func=ACT.Square, bias=negmu[:, ic], scale=1.0, accum_out=ssq[:, ic]
@@ -159,19 +162,20 @@ def tile_multiheadattention_pb_kernel(tc, attn_out, residual, proj_w, proj_b, ln
                 out=y_sb[i][:, VD:D], in_=y_sb[i][:, VD:D], func=ACT.Identity, scale=rstd[:, ic], bias=nmr[:, ic]
             )
 
-        def direct(i):
-            ic = slice(i, i + 1)
-            y = y_sb[i]
-            for c in range(VD // CH):
-                cs = slice(c * CH, (c + 1) * CH)
-                nc.vector.scalar_tensor_tensor(
-                    out=y[:, cs], in0=y[:, cs], scalar=negmu[:, ic], in1=g_ps[:, cs], op0=ALU.add, op1=ALU.mult
-                )
-            for c in range(VD // CH):
-                cs = slice(c * CH, (c + 1) * CH)
-                nc.vector.scalar_tensor_tensor(
-                    out=o_sb[i][:, cs], in0=y[:, cs], scalar=rstd[:, ic], in1=be_ps[:, cs], op0=ALU.mult, op1=ALU.add
-                )
+        def direct_gain(i):
+            nc.vector.scalar_tensor_tensor(
+                out=y_sb[i][:, 0:VD], in0=y_sb[i][:, 0:VD], scalar=negmu[:, i:i + 1], in1=g_ps[:], op0=ALU.add,
+                op1=ALU.mult,
+            )
+
+        def direct_bias(i):
+            nc.vector.scalar_tensor_tensor(
+                out=o_sb[i][:, 0:VD], in0=y_sb[i][:, 0:VD], scalar=rstd[:, i:i + 1], in1=be_ps[:], op0=ALU.mult,
+                op1=ALU.add,
+            )
+            nc.sync.dma_start(out=o0_view[i][:, 0:VD], in_=o_sb[i][:, 0:VD])
+
+        def direct_absmax(i):
             nc.vector.tensor_reduce(
                 out=am[:, i * NCH:i * NCH + 1], in_=o_sb[i][:, 0:VD], axis=AX.X, op=ALU.max, apply_absolute_value=True
             )
@@ -212,22 +216,20 @@ def tile_multiheadattention_pb_kernel(tc, attn_out, residual, proj_w, proj_b, ln
 
         def copy_out(u):
             q, h = divmod(u, NU)
-            for e in range(2):
-                c0 = VD + h * CH
-                nc.scalar.copy(out=o_sb[2 * q + e][:, c0:c0 + CH], in_=t2_ps[u][e][:])
-
-        def unit_absmax(u):
-            q, h = divmod(u, NU)
+            c0 = VD + h * CH
             for e in range(2):
                 i = 2 * q + e
-                c0 = VD + h * CH
-                k = i * NCH + VD // CH + h
-                nc.vector.tensor_reduce(
-                    out=am[:, k:k + 1], in_=o_sb[i][:, c0:c0 + CH], axis=AX.X, op=ALU.max, apply_absolute_value=True
-                )
-            if h == NU - 1:
-                for e in range(2):
-                    nc.sync.dma_start(out=o0_view[2 * q + e], in_=o_sb[2 * q + e][:])
+                nc.scalar.copy(out=o_sb[i][:, c0:c0 + CH], in_=t2_ps[u][e][:])
+                nc.sync.dma_start(out=o0_view[i][:, c0:c0 + CH], in_=o_sb[i][:, c0:c0 + CH])
+
+        def unit_absmax(u, e):
+            q, h = divmod(u, NU)
+            i = 2 * q + e
+            c0 = VD + h * CH
+            k = i * NCH + VD // CH + h
+            nc.vector.tensor_reduce(
+                out=am[:, k:k + 1], in_=o_sb[i][:, c0:c0 + CH], axis=AX.X, op=ALU.max, apply_absolute_value=True
+            )
 
         with tc.tile_pool(name="wpool", bufs=1) as wpool:
             w_raw = []
@@ -285,19 +287,23 @@ def tile_multiheadattention_pb_kernel(tc, attn_out, residual, proj_w, proj_b, ln
             x_copy(0)
             x_quantise(0, 1)
 
-            for c in range(NCH):
+            def spread_bias(c):
                 cs = slice(c * CH, (c + 1) * CH)
                 pb = psum.tile([P, CH], F32, name="pb", tag="t1")
                 nc.tensor.matmul(out=pb[:], lhsT=ones_b[:], rhs=rows[:, cs], start=True, stop=True)
-                nc.scalar.copy(out=b_bc[:, cs], in_=pb[:])
-            add_bias(0, 4)
+                nc.vector.tensor_copy(out=b_bc[:, cs], in_=pb[:])
+                add_bias_piece(0, c, NCH)
 
             w_interleave(0, "vector")
             w_quantise(0)
             w_interleave(1, "scalar")
+            spread_bias(0)
+            spread_bias(1)
             w_interleave(2, "vector")
             w_quantise(2)
             w_interleave(3, "scalar")
+            spread_bias(2)
+            spread_bias(3)
             w_quantise(1)
             w_quantise(3)
 
@@ -351,16 +357,22 @@ def tile_multiheadattention_pb_kernel(tc, attn_out, residual, proj_w, proj_b, ln
             if t >= 1:
                 to_tokens(t - 1)
             to_features(t)
-            direct(t)
+            direct_gain(t)
+            if t >= 2:
+                unit_absmax(t - 2, 0)
+            direct_bias(t)
+            if t >= 2:
+                unit_absmax(t - 2, 1)
+            direct_absmax(t)
             if t >= 1:
                 copy_out(t - 1)
-            if t >= 2:
-                unit_absmax(t - 2)
         gain_bias(NT - 1)
         to_tokens(NT - 1)
-        unit_absmax(NT - 2)
+        unit_absmax(NT - 2, 0)
+        unit_absmax(NT - 2, 1)
         copy_out(NT - 1)
-        unit_absmax(NT - 1)
+        unit_absmax(NT - 1, 0)
+        unit_absmax(NT - 1, 1)
 
         pm = keep.tile([P, 1], F32, name="pm")
         nc.vector.tensor_reduce(out=pm[:], in_=am[:], axis=AX.X, op=ALU.max)

@@ -30,6 +30,7 @@ NJ = D // P
 VD = 1024
 NU = (D - VD) // CH
 R_BUFS = 4
+G_NORM = 4
 
 
 def tile_multiheadattention_pb_kernel(tc, attn_out, residual, proj_w, proj_b, ln_g, ln_b, out_0, out_1):
@@ -65,10 +66,12 @@ def tile_multiheadattention_pb_kernel(tc, attn_out, residual, proj_w, proj_b, ln
         sums_s = keep.tile([P, NT, NCH], F32, name="sums_s")
         negmu = keep.tile([P, NT], F32, name="negmu")
         ssq = keep.tile([P, NT], F32, name="ssq")
-        sd = keep.tile([P, NT], F32, name="sd")
         rstd = keep.tile([P, NT], F32, name="rstd")
         nmr = keep.tile([P, NT], F32, name="nmr")
         am = keep.tile([P, NT * NCH], F32, name="am")
+        bsum = keep.tile([P, 2], F32, name="bsum")
+        bsum_s = keep.tile([P, 2], F32, name="bsum_s")
+        nbq = keep.tile([P, 1], F32, name="nbq")
         gb_col = keep.tile([P, 2 * NJ], F32, name="gb_col")
         xg = keep.tile([P, NT * P * 4], BF16, name="xg", align_bytes=64)
         x_codes = keep.tile([P, NT * P], U32, name="x_codes", align_bytes=64)
@@ -78,6 +81,7 @@ def tile_multiheadattention_pb_kernel(tc, attn_out, residual, proj_w, proj_b, ln
 
         r_sb = {}
         y_sb = {}
+        acc_ps = {}
         xt_ps = {}
         t1_ps = {}
         t2_ps = {}
@@ -113,50 +117,61 @@ def tile_multiheadattention_pb_kernel(tc, attn_out, residual, proj_w, proj_b, ln
                 in_=xg[:, a * 1024:(a + n) * 1024],
             )
 
-        def add_bias_piece(i, k, pieces):
-            if k == 0:
+        def project_chunk(i, c):
+            if c == 0:
                 y_sb[i] = work.tile([P, D], F32, name="y", tag="y")
-            w = D // pieces
-            ks = slice(k * w, (k + 1) * w)
-            nc.gpsimd.tensor_tensor(out=y_sb[i][:, ks], in0=r_sb[i][:, ks], in1=b_bc[:, ks], op=ALU.add)
+            acc = psum.tile([P, CH], F32, name="acc", tag="mm", bufs=4)
+            nc.tensor.matmul_mx(
+                out=acc[:],
+                lhsT=x_codes[:, i * P:(i + 1) * P].bitcast(FP8X4),
+                lhsT_scale=x_scales[:, i * P:(i + 1) * P],
+                rhs=w_codes[c][:].bitcast(FP8X4),
+                rhs_scale=w_scales[c][:],
+                start=True,
+                stop=True,
+            )
+            acc_ps[(i, c)] = acc
 
-        def add_bias(i, pieces):
-            for k in range(pieces):
-                add_bias_piece(i, k, pieces)
+        def add_residual_chunk(i, c):
+            cs = slice(c * CH, (c + 1) * CH)
+            nc.vector.scalar_tensor_tensor(
+                out=y_sb[i][:, cs], in0=acc_ps[(i, c)][:], scalar=1.0, in1=r_sb[i][:, cs], op0=ALU.mult, op1=ALU.add,
+                accum_out=sums[:, i, c:c + 1],
+            )
 
         def project(i):
-            y = y_sb[i]
             for c in range(NCH):
-                acc = psum.tile([P, CH], F32, name="acc", tag="mm", bufs=4)
-                nc.tensor.matmul_mx(
-                    out=acc[:],
-                    lhsT=x_codes[:, i * P:(i + 1) * P].bitcast(FP8X4),
-                    lhsT_scale=x_scales[:, i * P:(i + 1) * P],
-                    rhs=w_codes[c][:].bitcast(FP8X4),
-                    rhs_scale=w_scales[c][:],
-                    start=True,
-                    stop=True,
-                )
-                cs = slice(c * CH, (c + 1) * CH)
-                nc.vector.scalar_tensor_tensor(
-                    out=y[:, cs], in0=acc[:], scalar=1.0, in1=y[:, cs], op0=ALU.mult, op1=ALU.add,
-                    accum_out=sums[:, i, c:c + 1],
-                )
+                project_chunk(i, c)
+                add_residual_chunk(i, c)
+
+        def add_bias(i, pieces):
+            w = D // pieces
+            for k in range(pieces):
+                ks = slice(k * w, (k + 1) * w)
+                nc.gpsimd.tensor_tensor(out=y_sb[i][:, ks], in0=y_sb[i][:, ks], in1=b_bc[:, ks], op=ALU.add)
 
         def variance(i):
             ic = slice(i, i + 1)
             nc.scalar.activation(
-                out=sums_s[:, i, :], in_=sums[:, i, :], func=ACT.Copy, scale=-1.0 / D, accum_out=negmu[:, ic]
+                out=sums_s[:, i, :], in_=sums[:, i, :], func=ACT.Identity, scale=-1.0 / D, bias=nbq[:, 0:1],
+                accum_out=negmu[:, ic],
             )
             sq = late.tile([P, D], BF16, name="sq", tag="sq")
             nc.scalar.activation(
                 out=sq[:], in_=y_sb[i][:], func=ACT.Square, bias=negmu[:, ic], scale=1.0, accum_out=ssq[:, ic]
             )
-            nc.scalar.activation(out=sd[:, ic], in_=ssq[:, ic], func=ACT.Sqrt, bias=LN_EPS, scale=1.0 / D)
+            nc.scalar.activation(
+                out=rstd[:, ic], in_=ssq[:, ic], func=ACT.Abs_reciprocal_sqrt, bias=LN_EPS, scale=1.0 / D
+            )
 
         def normalise(i):
             ic = slice(i, i + 1)
-            nc.vector.reciprocal(out=rstd[:, ic], in_=sd[:, ic])
+            if i >= G_NORM:
+                nc.gpsimd.tensor_scalar(
+                    out=y_sb[i][:, VD:D], in0=y_sb[i][:, VD:D], scalar1=negmu[:, ic], scalar2=rstd[:, ic],
+                    op0=ALU.add, op1=ALU.mult,
+                )
+                return
             nc.scalar.activation(out=nmr[:, ic], in_=negmu[:, ic], func=ACT.Copy, scale=rstd[:, ic])
             nc.scalar.activation(
                 out=y_sb[i][:, VD:D], in_=y_sb[i][:, VD:D], func=ACT.Identity, scale=rstd[:, ic], bias=nmr[:, ic]
@@ -180,11 +195,11 @@ def tile_multiheadattention_pb_kernel(tc, attn_out, residual, proj_w, proj_b, ln
                 out=am[:, i * NCH:i * NCH + 1], in_=o_sb[i][:, 0:VD], axis=AX.X, op=ALU.max, apply_absolute_value=True
             )
 
-        def to_features(u):
+        def to_features(u, tag):
             q, h = divmod(u, NU)
             t1_ps[u] = []
             for s in range(2):
-                t1 = psum.tile([P, 2, 2, P], F32, name="t1", tag="t1")
+                t1 = psum.tile([P, 2, 2, P], F32, name="t1", tag=tag, bufs=4 if tag == "mm" else 2)
                 for jj in range(2):
                     c0 = VD + h * CH + (2 * s + jj) * P
                     for e in range(2):
@@ -264,19 +279,20 @@ def tile_multiheadattention_pb_kernel(tc, attn_out, residual, proj_w, proj_b, ln
             nc.vector.memset(am[:], 0.0)
             make_identity(nc, ident[:])
             make_identity(nc, ident_b[:])
-            nc.scalar.activation(out=warm[:], in_=ones[:], func=ACT.Sqrt)
+            nc.scalar.activation(out=warm[:], in_=ones[:], func=ACT.Abs_reciprocal_sqrt)
 
             load_x(0)
             load_x(1)
-            load_r(0)
             load_w(0)
+            load_w(1)
             nc.sync.dma_start(out=rows[0:1, 0:D], in_=proj_b.rearrange("(o d) -> o d", o=1))
             nc.sync.dma_start(out=rows[0:1, D:D + VD], in_=ln_g.rearrange("(o d) -> o d", o=1)[:, 0:VD])
             nc.sync.dma_start(out=rows[0:1, D + VD:D + 2 * VD], in_=ln_b.rearrange("(o d) -> o d", o=1)[:, 0:VD])
             nc.sync.dma_start(out=gb_rows[0:NJ, :], in_=ln_g.rearrange("(j p) -> j p", p=P))
             nc.sync.dma_start(out=gb_rows[NJ:2 * NJ, :], in_=ln_b.rearrange("(j p) -> j p", p=P))
-            for c in range(1, NCH):
-                load_w(c)
+            load_w(2)
+            load_w(3)
+            load_r(0)
             for i in range(2, NT):
                 load_x(i)
             load_r(1)
@@ -285,27 +301,10 @@ def tile_multiheadattention_pb_kernel(tc, attn_out, residual, proj_w, proj_b, ln
 
             x_transpose(0)
             x_copy(0)
-            x_quantise(0, 1)
-
-            def spread_bias(c):
-                cs = slice(c * CH, (c + 1) * CH)
-                pb = psum.tile([P, CH], F32, name="pb", tag="t1")
-                nc.tensor.matmul(out=pb[:], lhsT=ones_b[:], rhs=rows[:, cs], start=True, stop=True)
-                nc.vector.tensor_copy(out=b_bc[:, cs], in_=pb[:])
-                add_bias_piece(0, c, NCH)
-
             w_interleave(0, "vector")
-            w_quantise(0)
+            x_quantise(0, 1)
             w_interleave(1, "scalar")
-            spread_bias(0)
-            spread_bias(1)
-            w_interleave(2, "vector")
-            w_quantise(2)
-            w_interleave(3, "scalar")
-            spread_bias(2)
-            spread_bias(3)
-            w_quantise(1)
-            w_quantise(3)
+            w_quantise(0)
 
             for c in range(VD // CH):
                 cs = slice(c * CH, (c + 1) * CH)
@@ -316,63 +315,132 @@ def tile_multiheadattention_pb_kernel(tc, attn_out, residual, proj_w, proj_b, ln
                     out=be_ps[:, cs], lhsT=ones_b[:], rhs=rows[:, D + VD + c * CH:D + VD + (c + 1) * CH],
                     start=True, stop=True,
                 )
+            gbt = psum.tile([P, P], BF16, name="gbt", tag="t1")
+            nc.tensor.transpose(gbt[:], gb_rows[:], ident_b[:])
+            nc.vector.tensor_copy(out=gb_col[:], in_=gbt[:, 0:2 * NJ])
+            pb = []
+            for k in range(2):
+                pb.append(psum.tile([P, 2 * CH], BF16, name="pb", tag="t1"))
+                for c in range(2):
+                    nc.tensor.matmul(
+                        out=pb[k][:, c * CH:(c + 1) * CH], lhsT=ones_b[:],
+                        rhs=rows[:, (2 * k + c) * CH:(2 * k + c + 1) * CH], start=True, stop=True,
+                    )
+
+            w_interleave(2, "vector")
+            w_interleave(3, "scalar")
+            w_quantise(1)
+            w_quantise(2)
+            project_chunk(0, 0)
+            project_chunk(0, 1)
+            project_chunk(0, 2)
+            add_residual_chunk(0, 0)
+            add_residual_chunk(0, 1)
+            w_quantise(3)
+            add_residual_chunk(0, 2)
+            for a in range(1, NT // 2):
+                x_transpose(a)
+                x_copy(a)
+            project_chunk(0, 3)
+            add_residual_chunk(0, 3)
+            x_quantise(1, 1)
+            x_quantise(2, 2)
+            for k in range(2):
+                nc.scalar.activation(
+                    out=b_bc[:, 2 * k * CH:2 * (k + 1) * CH], in_=pb[k][:], func=ACT.Copy, accum_out=bsum[:, k:k + 1]
+                )
+            nc.scalar.activation(out=bsum_s[:], in_=bsum[:], func=ACT.Copy, scale=-1.0 / (NCH * D), accum_out=nbq[:])
 
         late = ctx.enter_context(tc.tile_pool(name="late", bufs=2))
 
-        gbt = psum.tile([P, P], BF16, name="gbt", tag="t1")
-        nc.tensor.transpose(gbt[:], gb_rows[:], ident_b[:])
-        nc.vector.tensor_copy(out=gb_col[:], in_=gbt[:, 0:2 * NJ])
+        def sums_of(i):
+            project(i)
+            add_bias(i, 1)
+            if i + R_BUFS < NT:
+                load_r(i + R_BUFS)
 
-        add_bias(1, 4)
-        load_r(4)
-        load_r(5)
-        for a in range(1, NT // 2):
-            x_transpose(a)
-            x_copy(a)
-        project(0)
+        def direct_step(k):
+            if k < NT:
+                direct_gain(k)
+            if 0 <= k - 1 < NT:
+                direct_bias(k - 1)
+            if 0 <= k - 2 < NT:
+                direct_absmax(k - 2)
+            if 0 <= k - 3 < G_NORM:
+                unit_absmax(k - 3, 0)
+                unit_absmax(k - 3, 1)
+
+        add_bias(0, 2)
+        load_r(R_BUFS)
+        sums_of(1)
+        sums_of(2)
+
         variance(0)
-        x_quantise(1, 1)
-        x_quantise(2, 2)
-        add_bias(2, 1)
-        load_r(6)
-        project(1)
-        variance(1)
-        add_bias(3, 1)
-        load_r(7)
         normalise(0)
+        sums_of(3)
+        sums_of(4)
 
-        for t in range(NT):
-            if 0 < t < NT - 1:
-                normalise(t + 1)
-            if t + 4 < NT:
-                add_bias(t + 4, 1)
-            if t + 2 < NT:
-                project(t + 2)
-            if t == 0:
-                normalise(1)
-            if t >= 1:
-                gain_bias(t - 1)
-            if t + 2 < NT:
-                variance(t + 2)
-            if t >= 1:
-                to_tokens(t - 1)
-            to_features(t)
-            direct_gain(t)
-            if t >= 2:
-                unit_absmax(t - 2, 0)
-            direct_bias(t)
-            if t >= 2:
-                unit_absmax(t - 2, 1)
-            direct_absmax(t)
-            if t >= 1:
-                copy_out(t - 1)
-        gain_bias(NT - 1)
-        to_tokens(NT - 1)
-        unit_absmax(NT - 2, 0)
-        unit_absmax(NT - 2, 1)
-        copy_out(NT - 1)
-        unit_absmax(NT - 1, 0)
-        unit_absmax(NT - 1, 1)
+        variance(1)
+        normalise(1)
+        sums_of(5)
+        sums_of(6)
+        to_features(0, "t1")
+        sums_of(7)
+
+        variance(2)
+        gain_bias(0)
+        to_tokens(0)
+        to_features(1, "t1")
+        normalise(2)
+        copy_out(0)
+
+        variance(3)
+        gain_bias(1)
+        to_tokens(1)
+        normalise(3)
+        to_features(2, "t1")
+        copy_out(1)
+        direct_step(0)
+        direct_step(1)
+
+        gain_bias(2)
+        to_tokens(2)
+        to_features(3, "t1")
+        variance(4)
+        normalise(4)
+        copy_out(2)
+        direct_step(2)
+        direct_step(3)
+
+        gain_bias(3)
+        to_tokens(3)
+        variance(5)
+        normalise(5)
+        copy_out(3)
+        direct_step(4)
+        direct_step(5)
+
+        variance(6)
+        normalise(6)
+        direct_step(6)
+        variance(7)
+        normalise(7)
+        direct_step(7)
+
+        for q in (2, 3):
+            a = 2 * q
+            to_features(a, "t1")
+            to_features(a + 1, "mm")
+            gain_bias(a)
+            to_tokens(a)
+            gain_bias(a + 1)
+            to_tokens(a + 1)
+            copy_out(a)
+            copy_out(a + 1)
+            direct_step(NT + q - 2)
+        for u in range(G_NORM, NT):
+            unit_absmax(u, 0)
+            unit_absmax(u, 1)
 
         pm = keep.tile([P, 1], F32, name="pm")
         nc.vector.tensor_reduce(out=pm[:], in_=am[:], axis=AX.X, op=ALU.max)

@@ -28,7 +28,7 @@ FLOPS = 2 * LQ * K * D
 CAST_V = 1344
 NJ = D // P
 VD = 1024
-NU = (D - VD) // CH
+VDQ = (1024, 1024, 1024, 1024)
 R_BUFS = 4
 G_NORM = 4
 
@@ -166,53 +166,57 @@ def tile_multiheadattention_pb_kernel(tc, attn_out, residual, proj_w, proj_b, ln
 
         def normalise(i):
             ic = slice(i, i + 1)
+            vd = VDQ[i // 2]
             if i >= G_NORM:
                 nc.gpsimd.tensor_scalar(
-                    out=y_sb[i][:, VD:D], in0=y_sb[i][:, VD:D], scalar1=negmu[:, ic], scalar2=rstd[:, ic],
+                    out=y_sb[i][:, vd:D], in0=y_sb[i][:, vd:D], scalar1=negmu[:, ic], scalar2=rstd[:, ic],
                     op0=ALU.add, op1=ALU.mult,
                 )
                 return
             nc.scalar.activation(out=nmr[:, ic], in_=negmu[:, ic], func=ACT.Copy, scale=rstd[:, ic])
             nc.scalar.activation(
-                out=y_sb[i][:, VD:D], in_=y_sb[i][:, VD:D], func=ACT.Identity, scale=rstd[:, ic], bias=nmr[:, ic]
+                out=y_sb[i][:, vd:D], in_=y_sb[i][:, vd:D], func=ACT.Identity, scale=rstd[:, ic], bias=nmr[:, ic]
             )
 
         def direct_gain(i):
+            vd = VDQ[i // 2]
             nc.vector.scalar_tensor_tensor(
-                out=y_sb[i][:, 0:VD], in0=y_sb[i][:, 0:VD], scalar=negmu[:, i:i + 1], in1=g_ps[:], op0=ALU.add,
+                out=y_sb[i][:, 0:vd], in0=y_sb[i][:, 0:vd], scalar=negmu[:, i:i + 1], in1=g_ps[:, 0:vd], op0=ALU.add,
                 op1=ALU.mult,
             )
 
         def direct_bias(i):
+            vd = VDQ[i // 2]
             nc.vector.scalar_tensor_tensor(
-                out=o_sb[i][:, 0:VD], in0=y_sb[i][:, 0:VD], scalar=rstd[:, i:i + 1], in1=be_ps[:], op0=ALU.mult,
+                out=o_sb[i][:, 0:vd], in0=y_sb[i][:, 0:vd], scalar=rstd[:, i:i + 1], in1=be_ps[:, 0:vd], op0=ALU.mult,
                 op1=ALU.add,
             )
-            nc.sync.dma_start(out=o0_view[i][:, 0:VD], in_=o_sb[i][:, 0:VD])
+            nc.sync.dma_start(out=o0_view[i][:, 0:vd], in_=o_sb[i][:, 0:vd])
 
         def direct_absmax(i):
+            vd = VDQ[i // 2]
             nc.vector.tensor_reduce(
-                out=am[:, i * NCH:i * NCH + 1], in_=o_sb[i][:, 0:VD], axis=AX.X, op=ALU.max, apply_absolute_value=True
+                out=am[:, i * NCH:i * NCH + 1], in_=o_sb[i][:, 0:vd], axis=AX.X, op=ALU.max, apply_absolute_value=True
             )
 
         def to_features(u, tag):
-            q, h = divmod(u, NU)
+            q, c = u
             t1_ps[u] = []
             for s in range(2):
                 t1 = psum.tile([P, 2, 2, P], F32, name="t1", tag=tag, bufs=4 if tag == "mm" else 2)
                 for jj in range(2):
-                    c0 = VD + h * CH + (2 * s + jj) * P
+                    c0 = c * CH + (2 * s + jj) * P
                     for e in range(2):
                         nc.tensor.transpose(t1[:, jj, e, :], y_sb[2 * q + e][:, c0:c0 + P], ident[:])
                 t1_ps[u].append(t1)
 
         def gain_bias(u):
-            q, h = divmod(u, NU)
+            q, c = u
             ot_sb[u] = []
             for s in range(2):
                 ot = late.tile([P, 2, 2, P], F32, name="ot", tag="ot", bufs=4)
                 for jj in range(2):
-                    j = (VD + h * CH) // P + 2 * s + jj
+                    j = c * CH // P + 2 * s + jj
                     nc.scalar.activation(
                         out=ot[:, jj, :, :], in_=t1_ps[u][s][:, jj, :, :], func=ACT.Identity,
                         scale=gb_col[:, j:j + 1], bias=gb_col[:, NJ + j:NJ + j + 1],
@@ -230,21 +234,20 @@ def tile_multiheadattention_pb_kernel(tc, attn_out, residual, proj_w, proj_b, ln
                         nc.tensor.transpose(t2_ps[u][e][:, k * P:(k + 1) * P], ot_sb[u][s][:, jj, e, :], ident[:])
 
         def copy_out(u):
-            q, h = divmod(u, NU)
-            c0 = VD + h * CH
+            q, c = u
             for e in range(2):
                 i = 2 * q + e
-                nc.scalar.copy(out=o_sb[i][:, c0:c0 + CH], in_=t2_ps[u][e][:])
-                nc.sync.dma_start(out=o0_view[i][:, c0:c0 + CH], in_=o_sb[i][:, c0:c0 + CH])
+                nc.scalar.copy(out=o_sb[i][:, c * CH:(c + 1) * CH], in_=t2_ps[u][e][:])
+                nc.sync.dma_start(out=o0_view[i][:, c * CH:(c + 1) * CH], in_=o_sb[i][:, c * CH:(c + 1) * CH])
 
-        def unit_absmax(u, e):
-            q, h = divmod(u, NU)
-            i = 2 * q + e
-            c0 = VD + h * CH
-            k = i * NCH + VD // CH + h
-            nc.vector.tensor_reduce(
-                out=am[:, k:k + 1], in_=o_sb[i][:, c0:c0 + CH], axis=AX.X, op=ALU.max, apply_absolute_value=True
-            )
+        def unit_absmax(u):
+            q, c = u
+            for e in range(2):
+                i = 2 * q + e
+                nc.vector.tensor_reduce(
+                    out=am[:, i * NCH + c:i * NCH + c + 1], in_=o_sb[i][:, c * CH:(c + 1) * CH], axis=AX.X, op=ALU.max,
+                    apply_absolute_value=True,
+                )
 
         with tc.tile_pool(name="wpool", bufs=1) as wpool:
             w_raw = []
@@ -342,8 +345,8 @@ def tile_multiheadattention_pb_kernel(tc, attn_out, residual, proj_w, proj_b, ln
                 x_transpose(a)
                 x_copy(a)
             project_chunk(0, 3)
-            add_residual_chunk(0, 3)
             x_quantise(1, 1)
+            add_residual_chunk(0, 3)
             x_quantise(2, 2)
             for k in range(2):
                 nc.scalar.activation(
@@ -359,16 +362,24 @@ def tile_multiheadattention_pb_kernel(tc, attn_out, residual, proj_w, proj_b, ln
             if i + R_BUFS < NT:
                 load_r(i + R_BUFS)
 
+        units = []
+        for q in range(NT // 2):
+            for c in range(VDQ[q] // CH, NCH):
+                units.append((q, c))
+        early = [u for u in units if 2 * u[0] < G_NORM]
+        tail = [u for u in units if 2 * u[0] >= G_NORM]
+
         def direct_step(k):
-            if k < NT:
+            if k < 3:
                 direct_gain(k)
             if 0 <= k - 1 < NT:
                 direct_bias(k - 1)
+            if 0 <= k - 3 < len(early):
+                unit_absmax(early[k - 3])
+            if 3 <= k < NT:
+                direct_gain(k)
             if 0 <= k - 2 < NT:
                 direct_absmax(k - 2)
-            if 0 <= k - 3 < G_NORM:
-                unit_absmax(k - 3, 0)
-                unit_absmax(k - 3, 1)
 
         add_bias(0, 2)
         load_r(R_BUFS)
@@ -384,74 +395,73 @@ def tile_multiheadattention_pb_kernel(tc, attn_out, residual, proj_w, proj_b, ln
         normalise(1)
         sums_of(5)
         sums_of(6)
-        to_features(0, "t1")
+        to_features(early[0], "t1")
         sums_of(7)
 
         variance(2)
-        gain_bias(0)
-        to_tokens(0)
-        to_features(1, "t1")
+        gain_bias(early[0])
+        to_tokens(early[0])
+        to_features(early[1], "t1")
         normalise(2)
-        copy_out(0)
+        copy_out(early[0])
 
         variance(3)
-        gain_bias(1)
-        to_tokens(1)
+        gain_bias(early[1])
+        to_tokens(early[1])
         normalise(3)
-        to_features(2, "t1")
-        copy_out(1)
+        to_features(early[2], "t1")
+        copy_out(early[1])
         direct_step(0)
         direct_step(1)
 
-        gain_bias(2)
-        to_tokens(2)
-        to_features(3, "t1")
         variance(4)
         normalise(4)
-        copy_out(2)
+        gain_bias(early[2])
+        to_tokens(early[2])
+        to_features(early[3], "t1")
         direct_step(2)
         direct_step(3)
-
-        gain_bias(3)
-        to_tokens(3)
+        direct_step(4)
         variance(5)
         normalise(5)
-        copy_out(3)
-        direct_step(4)
+        copy_out(early[2])
+        gain_bias(early[3])
+        to_tokens(early[3])
         direct_step(5)
-
         variance(6)
         normalise(6)
+        copy_out(early[3])
         direct_step(6)
         variance(7)
         normalise(7)
         direct_step(7)
 
-        for q in (2, 3):
-            a = 2 * q
-            to_features(a, "t1")
-            to_features(a + 1, "mm")
-            gain_bias(a)
-            to_tokens(a)
-            gain_bias(a + 1)
-            to_tokens(a + 1)
-            copy_out(a)
-            copy_out(a + 1)
-            direct_step(NT + q - 2)
-        for u in range(G_NORM, NT):
-            unit_absmax(u, 0)
-            unit_absmax(u, 1)
+        n = len(tail)
+        for k in range(n + 2):
+            if k < n:
+                to_features(tail[k], "t1" if k % 2 == 0 else "mm")
+            if 0 <= k - 1 < n:
+                gain_bias(tail[k - 1])
+            if 0 <= k - 2 < n:
+                copy_out(tail[k - 2])
+            if 0 <= k - 1 < n:
+                to_tokens(tail[k - 1])
+            if k < 2:
+                direct_step(NT + k)
+        for u in tail:
+            unit_absmax(u)
 
         pm = keep.tile([P, 1], F32, name="pm")
-        nc.vector.tensor_reduce(out=pm[:], in_=am[:], axis=AX.X, op=ALU.max)
+        am_s = keep.tile([P, NT * NCH], F32, name="am_s")
+        nc.vector.tensor_scalar(
+            out=am_s[:], in0=am[:], scalar1=1.0 / 448.0, scalar2=None, op0=ALU.mult, op1=ALU.max, accum_out=pm[:]
+        )
         pt = psum.tile([P, P], F32, name="pt", tag="t1")
         nc.tensor.transpose(pt[:], pm[:, 0:1].to_broadcast([P, P]), ident[:])
         gm = keep.tile([P, 1], F32, name="gm")
         nc.vector.tensor_reduce(out=gm[:], in_=pt[:], axis=AX.X, op=ALU.max)
-        rc = keep.tile([P, 1], F32, name="rc")
-        nc.vector.reciprocal(out=rc[:], in_=gm[:])
         fac = keep.tile([P, 1], F32, name="fac")
-        nc.vector.tensor_scalar(out=fac[:], in0=rc[:], scalar1=448.0, scalar2=None, op0=ALU.mult)
+        nc.vector.reciprocal(out=fac[:], in_=gm[:])
 
         for i in range(NT):
             f8 = work.tile([P, D], FP8, name="f8", tag="y")

@@ -150,30 +150,38 @@ def tile_multiheadattention_pb_kernel(tc, attn_out, residual, proj_w, proj_b, ln
                 ks = slice(k * w, (k + 1) * w)
                 nc.gpsimd.tensor_tensor(out=y_sb[i][:, ks], in0=y_sb[i][:, ks], in1=b_bc[:, ks], op=ALU.add)
 
-        def variance(i):
-            ic = slice(i, i + 1)
+        def mean_of(i):
             nc.scalar.activation(
                 out=sums_s[:, i, :], in_=sums[:, i, :], func=ACT.Identity, scale=-1.0 / D, bias=nbq[:, 0:1],
-                accum_out=negmu[:, ic],
+                accum_out=negmu[:, i:i + 1],
             )
+
+        def squares(i):
             sq = late.tile([P, D], BF16, name="sq", tag="sq")
             nc.scalar.activation(
-                out=sq[:], in_=y_sb[i][:], func=ACT.Square, bias=negmu[:, ic], scale=1.0, accum_out=ssq[:, ic]
+                out=sq[:], in_=y_sb[i][:], func=ACT.Square, bias=negmu[:, i:i + 1], scale=1.0,
+                accum_out=ssq[:, i:i + 1],
             )
+
+        def inv_sd(i):
+            ic = slice(i, i + 1)
             nc.scalar.activation(
                 out=rstd[:, ic], in_=ssq[:, ic], func=ACT.Abs_reciprocal_sqrt, bias=LN_EPS, scale=1.0 / D
             )
-
-        def normalise(i):
-            ic = slice(i, i + 1)
-            vd = VDQ[i // 2]
             if i >= G_NORM:
+                vd = VDQ[i // 2]
                 nc.gpsimd.tensor_scalar(
                     out=y_sb[i][:, vd:D], in0=y_sb[i][:, vd:D], scalar1=negmu[:, ic], scalar2=rstd[:, ic],
                     op0=ALU.add, op1=ALU.mult,
                 )
-                return
+
+        def shift_of(i):
+            ic = slice(i, i + 1)
             nc.scalar.activation(out=nmr[:, ic], in_=negmu[:, ic], func=ACT.Copy, scale=rstd[:, ic])
+
+        def normalise(i):
+            ic = slice(i, i + 1)
+            vd = VDQ[i // 2]
             nc.scalar.activation(
                 out=y_sb[i][:, vd:D], in_=y_sb[i][:, vd:D], func=ACT.Identity, scale=rstd[:, ic], bias=nmr[:, ic]
             )
@@ -210,7 +218,7 @@ def tile_multiheadattention_pb_kernel(tc, attn_out, residual, proj_w, proj_b, ln
                         nc.tensor.transpose(t1[:, jj, e, :], y_sb[2 * q + e][:, c0:c0 + P], ident[:])
                 t1_ps[u].append(t1)
 
-        def gain_bias(u):
+        def gain_bias(u, between=()):
             q, c = u
             ot_sb[u] = []
             for s in range(2):
@@ -221,6 +229,9 @@ def tile_multiheadattention_pb_kernel(tc, attn_out, residual, proj_w, proj_b, ln
                         out=ot[:, jj, :, :], in_=t1_ps[u][s][:, jj, :, :], func=ACT.Identity,
                         scale=gb_col[:, j:j + 1], bias=gb_col[:, NJ + j:NJ + j + 1],
                     )
+                    if 2 * s + jj < len(between):
+                        f, i = between[2 * s + jj]
+                        f(i)
                 ot_sb[u].append(ot)
 
         def to_tokens(u):
@@ -233,12 +244,15 @@ def tile_multiheadattention_pb_kernel(tc, attn_out, residual, proj_w, proj_b, ln
                         k = 2 * s + jj
                         nc.tensor.transpose(t2_ps[u][e][:, k * P:(k + 1) * P], ot_sb[u][s][:, jj, e, :], ident[:])
 
-        def copy_out(u):
+        def copy_out(u, between=()):
             q, c = u
             for e in range(2):
                 i = 2 * q + e
                 nc.scalar.copy(out=o_sb[i][:, c * CH:(c + 1) * CH], in_=t2_ps[u][e][:])
                 nc.sync.dma_start(out=o0_view[i][:, c * CH:(c + 1) * CH], in_=o_sb[i][:, c * CH:(c + 1) * CH])
+                if e < len(between):
+                    f, k = between[e]
+                    f(k)
 
         def unit_absmax(u):
             q, c = u
@@ -386,55 +400,59 @@ def tile_multiheadattention_pb_kernel(tc, attn_out, residual, proj_w, proj_b, ln
         sums_of(1)
         sums_of(2)
 
-        variance(0)
+        mean_of(0)
+        squares(0)
+        mean_of(1)
+        inv_sd(0)
+        shift_of(0)
         normalise(0)
         sums_of(3)
         sums_of(4)
 
-        variance(1)
+        squares(1)
+        mean_of(2)
+        inv_sd(1)
+        shift_of(1)
         normalise(1)
         sums_of(5)
         sums_of(6)
         to_features(early[0], "t1")
         sums_of(7)
 
-        variance(2)
-        gain_bias(early[0])
+        squares(2)
+        gain_bias(early[0], ((inv_sd, 2), (shift_of, 2)))
         to_tokens(early[0])
         to_features(early[1], "t1")
         normalise(2)
-        copy_out(early[0])
+        copy_out(early[0], ((mean_of, 3),))
 
-        variance(3)
-        gain_bias(early[1])
+        squares(3)
+        gain_bias(early[1], ((inv_sd, 3), (shift_of, 3)))
         to_tokens(early[1])
         normalise(3)
         to_features(early[2], "t1")
-        copy_out(early[1])
+        copy_out(early[1], ((mean_of, 4),))
         direct_step(0)
         direct_step(1)
 
-        variance(4)
-        normalise(4)
-        gain_bias(early[2])
+        squares(4)
+        gain_bias(early[2], ((inv_sd, 4), (mean_of, 5)))
         to_tokens(early[2])
         to_features(early[3], "t1")
         direct_step(2)
         direct_step(3)
         direct_step(4)
-        variance(5)
-        normalise(5)
-        copy_out(early[2])
-        gain_bias(early[3])
+        squares(5)
+        copy_out(early[2], ((inv_sd, 5),))
+        mean_of(6)
+        gain_bias(early[3], ((mean_of, 7),))
         to_tokens(early[3])
         direct_step(5)
-        variance(6)
-        normalise(6)
-        copy_out(early[3])
+        squares(6)
+        copy_out(early[3], ((inv_sd, 6),))
         direct_step(6)
-        variance(7)
-        normalise(7)
-        direct_step(7)
+        squares(7)
+        inv_sd(7)
 
         n = len(tail)
         for k in range(n + 2):
@@ -446,8 +464,8 @@ def tile_multiheadattention_pb_kernel(tc, attn_out, residual, proj_w, proj_b, ln
                 copy_out(tail[k - 2])
             if 0 <= k - 1 < n:
                 to_tokens(tail[k - 1])
-            if k < 2:
-                direct_step(NT + k)
+            if k < 3:
+                direct_step(NT - 1 + k)
         for u in tail:
             unit_absmax(u)
 

@@ -30,6 +30,7 @@ NJ = D // P
 VD = 1024
 VDQ = (1024, 1024, 1024, 1024)
 R_BUFS = 4
+GD_TILES = (7,)
 G_NORM = 4
 
 
@@ -69,8 +70,9 @@ def tile_multiheadattention_pb_kernel(tc, attn_out, residual, proj_w, proj_b, ln
         rstd = keep.tile([P, NT], F32, name="rstd")
         nmr = keep.tile([P, NT], F32, name="nmr")
         am = keep.tile([P, NT * NCH], F32, name="am")
-        bsum = keep.tile([P, 2], F32, name="bsum")
-        bsum_s = keep.tile([P, 2], F32, name="bsum_s")
+        g_bc = keep.tile([P, VD], BF16, name="g_bc")
+        be_bc = keep.tile([P, VD], BF16, name="be_bc")
+        bsum = keep.tile([P, 1], F32, name="bsum")
         nbq = keep.tile([P, 1], F32, name="nbq")
         gb_col = keep.tile([P, 2 * NJ], F32, name="gb_col")
         xg = keep.tile([P, NT * P * 4], BF16, name="xg", align_bytes=64)
@@ -186,8 +188,20 @@ def tile_multiheadattention_pb_kernel(tc, attn_out, residual, proj_w, proj_b, ln
                 out=y_sb[i][:, vd:D], in_=y_sb[i][:, vd:D], func=ACT.Identity, scale=rstd[:, ic], bias=nmr[:, ic]
             )
 
+        def gpsimd_direct(i):
+            ic = slice(i, i + 1)
+            vd = VDQ[i // 2]
+            nc.gpsimd.tensor_scalar(
+                out=y_sb[i][:, 0:vd], in0=y_sb[i][:, 0:vd], scalar1=negmu[:, ic], scalar2=rstd[:, ic],
+                op0=ALU.add, op1=ALU.mult,
+            )
+            nc.gpsimd.tensor_tensor(out=y_sb[i][:, 0:vd], in0=y_sb[i][:, 0:vd], in1=g_bc[:, 0:vd], op=ALU.mult)
+            nc.gpsimd.tensor_tensor(out=o_sb[i][:, 0:vd], in0=y_sb[i][:, 0:vd], in1=be_bc[:, 0:vd], op=ALU.add)
+
         def direct_gain(i):
             vd = VDQ[i // 2]
+            if i in GD_TILES:
+                return
             nc.vector.scalar_tensor_tensor(
                 out=y_sb[i][:, 0:vd], in0=y_sb[i][:, 0:vd], scalar=negmu[:, i:i + 1], in1=g_ps[:, 0:vd], op0=ALU.add,
                 op1=ALU.mult,
@@ -195,14 +209,20 @@ def tile_multiheadattention_pb_kernel(tc, attn_out, residual, proj_w, proj_b, ln
 
         def direct_bias(i):
             vd = VDQ[i // 2]
+            if i in GD_TILES:
+                return
             nc.vector.scalar_tensor_tensor(
                 out=o_sb[i][:, 0:vd], in0=y_sb[i][:, 0:vd], scalar=rstd[:, i:i + 1], in1=be_ps[:, 0:vd], op0=ALU.mult,
                 op1=ALU.add,
             )
             nc.sync.dma_start(out=o0_view[i][:, 0:vd], in_=o_sb[i][:, 0:vd])
 
-        def direct_absmax(i):
+        def direct_absmax(i, late=False):
             vd = VDQ[i // 2]
+            if (i in GD_TILES) != late:
+                return
+            if late:
+                nc.sync.dma_start(out=o0_view[i][:, 0:vd], in_=o_sb[i][:, 0:vd])
             nc.vector.tensor_reduce(
                 out=am[:, i * NCH:i * NCH + 1], in_=o_sb[i][:, 0:vd], axis=AX.X, op=ALU.max, apply_absolute_value=True
             )
@@ -363,10 +383,7 @@ def tile_multiheadattention_pb_kernel(tc, attn_out, residual, proj_w, proj_b, ln
             add_residual_chunk(0, 3)
             x_quantise(2, 2)
             for k in range(2):
-                nc.scalar.activation(
-                    out=b_bc[:, 2 * k * CH:2 * (k + 1) * CH], in_=pb[k][:], func=ACT.Copy, accum_out=bsum[:, k:k + 1]
-                )
-            nc.scalar.activation(out=bsum_s[:], in_=bsum[:], func=ACT.Copy, scale=-1.0 / (NCH * D), accum_out=nbq[:])
+                nc.scalar.copy(out=b_bc[:, 2 * k * CH:2 * (k + 1) * CH], in_=pb[k][:])
 
         late = ctx.enter_context(tc.tile_pool(name="late", bufs=2))
 
@@ -397,6 +414,9 @@ def tile_multiheadattention_pb_kernel(tc, attn_out, residual, proj_w, proj_b, ln
 
         add_bias(0, 2)
         load_r(R_BUFS)
+        b_junk = late.tile([P, D], BF16, name="b_junk", tag="sq")
+        nc.scalar.activation(out=b_junk[:], in_=b_bc[:], func=ACT.Copy, accum_out=bsum[:, 0:1])
+        nc.scalar.activation(out=nbq[:], in_=bsum[:, 0:1], func=ACT.Copy, scale=-1.0 / (NCH * D))
         sums_of(1)
         sums_of(2)
 
@@ -406,6 +426,8 @@ def tile_multiheadattention_pb_kernel(tc, attn_out, residual, proj_w, proj_b, ln
         inv_sd(0)
         shift_of(0)
         normalise(0)
+        nc.scalar.copy(out=g_bc[:], in_=g_ps[:])
+        nc.scalar.copy(out=be_bc[:], in_=be_ps[:])
         sums_of(3)
         sums_of(4)
 
@@ -453,6 +475,8 @@ def tile_multiheadattention_pb_kernel(tc, attn_out, residual, proj_w, proj_b, ln
         direct_step(6)
         squares(7)
         inv_sd(7)
+        for i in GD_TILES:
+            gpsimd_direct(i)
 
         n = len(tail)
         for k in range(n + 2):
@@ -468,6 +492,8 @@ def tile_multiheadattention_pb_kernel(tc, attn_out, residual, proj_w, proj_b, ln
                 direct_step(NT - 1 + k)
         for u in tail:
             unit_absmax(u)
+        for i in GD_TILES:
+            direct_absmax(i, True)
 
         pm = keep.tile([P, 1], F32, name="pm")
         am_s = keep.tile([P, NT * NCH], F32, name="am_s")

@@ -242,7 +242,7 @@ def tile_multiheadattention_pb_kernel(tc, attn_out, residual, proj_w, proj_b, ln
             q, c = u
             ot_sb[u] = []
             for s in range(2):
-                ot = late.tile([P, 2, 2, P], F32, name="ot", tag="ot", bufs=4)
+                ot = late.tile([P, 2, 2, P], F32, name="ot", tag="ot", bufs=8)
                 for jj in range(2):
                     j = c * CH // P + 2 * s + jj
                     nc.scalar.activation(
@@ -273,6 +273,15 @@ def tile_multiheadattention_pb_kernel(tc, attn_out, residual, proj_w, proj_b, ln
                 if e < len(between):
                     f, k = between[e]
                     f(k)
+
+        def unit_absmax_early(u):
+            q, c = u
+            for s in range(2):
+                i = 2 * q + s
+                nc.vector.tensor_reduce(
+                    out=am[:, i * NCH + c:i * NCH + c + 1], in_=ot_sb[u][s][:].rearrange("p a b r -> p (a b r)"), axis=AX.X,
+                    op=ALU.max, apply_absolute_value=True,
+                )
 
         def unit_absmax(u):
             q, c = u
@@ -308,7 +317,7 @@ def tile_multiheadattention_pb_kernel(tc, attn_out, residual, proj_w, proj_b, ln
                     out=w_codes[c][:].bitcast(FP8X4), scales=w_scales[c][:], in_=wg[c][:].rearrange("p w j -> p (w j)")
                 )
 
-            nc.vector.memset(rows[:], 0.0)
+            nc.vector.memset(rows[:].bitcast(F32), 0.0)
             nc.vector.memset(ones_b[:], 1.0)
             nc.vector.memset(gb_rows[:], 0.0)
             nc.vector.memset(ones[:], 1.0)
@@ -420,13 +429,13 @@ def tile_multiheadattention_pb_kernel(tc, attn_out, residual, proj_w, proj_b, ln
         sums_of(1)
         sums_of(2)
 
+        nc.scalar.copy(out=g_bc[:], in_=g_ps[:])
         mean_of(0)
         squares(0)
         mean_of(1)
         inv_sd(0)
         shift_of(0)
         normalise(0)
-        nc.scalar.copy(out=g_bc[:], in_=g_ps[:])
         nc.scalar.copy(out=be_bc[:], in_=be_ps[:])
         sums_of(3)
         sums_of(4)
@@ -438,8 +447,8 @@ def tile_multiheadattention_pb_kernel(tc, attn_out, residual, proj_w, proj_b, ln
         normalise(1)
         sums_of(5)
         sums_of(6)
-        to_features(early[0], "t1")
         sums_of(7)
+        to_features(early[0], "t1")
 
         squares(2)
         gain_bias(early[0], ((inv_sd, 2), (shift_of, 2)))
@@ -490,8 +499,8 @@ def tile_multiheadattention_pb_kernel(tc, attn_out, residual, proj_w, proj_b, ln
                 to_tokens(tail[k - 1])
             if k < 3:
                 direct_step(NT - 1 + k)
-        for u in tail:
-            unit_absmax(u)
+            if 0 <= k - 1 < n:
+                unit_absmax_early(tail[k - 1])
         for i in GD_TILES:
             direct_absmax(i, True)
 

@@ -457,20 +457,20 @@ def tile_multiheadattention_pb_kernel(tc, attn_out, residual, proj_w, proj_b, ln
         normalise(2)
         copy_out(early[0], ((mean_of, 3),))
 
+        direct_step(0)
+        direct_step(1)
+        direct_step(2)
         squares(3)
         gain_bias(early[1], ((inv_sd, 3), (shift_of, 3)))
         to_tokens(early[1])
         normalise(3)
         to_features(early[2], "t1")
         copy_out(early[1], ((mean_of, 4),))
-        direct_step(0)
-        direct_step(1)
 
         squares(4)
         gain_bias(early[2], ((inv_sd, 4), (mean_of, 5)))
         to_tokens(early[2])
         to_features(early[3], "t1")
-        direct_step(2)
         direct_step(3)
         direct_step(4)
         squares(5)

@@ -78,6 +78,7 @@ def tile_multiheadattention_pb_kernel(tc, attn_out, residual, proj_w, proj_b, ln
         xg = keep.tile([P, NT * P * 4], BF16, name="xg", align_bytes=64)
         x_codes = keep.tile([P, NT * P], U32, name="x_codes", align_bytes=64)
         x_scales = keep.tile([P, NT * P], U8, name="x_scales", align_bytes=64)
+        rows_gb = keep.tile([P, 2 * VD], BF16, name="rows_gb")
         g_ps = cpsum.tile([P, VD], BF16, name="g_ps")
         be_ps = cpsum.tile([P, VD], BF16, name="be_ps")
 
@@ -300,7 +301,7 @@ def tile_multiheadattention_pb_kernel(tc, attn_out, residual, proj_w, proj_b, ln
                 wg.append(wpool.tile([P, CH, 4], BF16, name="wg%d" % c, align_bytes=64))
                 w_codes.append(keep.tile([P, CH], U32, name="w_codes%d" % c, align_bytes=64))
                 w_scales.append(keep.tile([P, CH], U8, name="w_scales%d" % c, align_bytes=64))
-            rows = wpool.tile([P, D + 2 * VD], BF16, name="rows")
+            rows = wpool.tile([P, D], BF16, name="rows")
 
             def load_w(c):
                 nc.sync.dma_start(out=w_raw[c][:], in_=w_view[:, :, c * CH:(c + 1) * CH])
@@ -318,6 +319,7 @@ def tile_multiheadattention_pb_kernel(tc, attn_out, residual, proj_w, proj_b, ln
                 )
 
             nc.vector.memset(rows[:].bitcast(F32), 0.0)
+            nc.vector.memset(rows_gb[:].bitcast(F32), 0.0)
             nc.vector.memset(ones_b[:], 1.0)
             nc.vector.memset(gb_rows[:], 0.0)
             nc.vector.memset(ones[:], 1.0)
@@ -332,16 +334,16 @@ def tile_multiheadattention_pb_kernel(tc, attn_out, residual, proj_w, proj_b, ln
             load_w(0)
             load_w(1)
             nc.sync.dma_start(out=rows[0:1, 0:D], in_=proj_b.rearrange("(o d) -> o d", o=1))
-            nc.sync.dma_start(out=rows[0:1, D:D + VD], in_=ln_g.rearrange("(o d) -> o d", o=1)[:, 0:VD])
-            nc.sync.dma_start(out=rows[0:1, D + VD:D + 2 * VD], in_=ln_b.rearrange("(o d) -> o d", o=1)[:, 0:VD])
-            nc.sync.dma_start(out=gb_rows[0:NJ, :], in_=ln_g.rearrange("(j p) -> j p", p=P))
-            nc.sync.dma_start(out=gb_rows[NJ:2 * NJ, :], in_=ln_b.rearrange("(j p) -> j p", p=P))
             load_w(2)
             load_w(3)
             load_r(0)
             for i in range(2, NT):
                 load_x(i)
             load_r(1)
+            nc.sync.dma_start(out=rows_gb[0:1, 0:VD], in_=ln_g.rearrange("(o d) -> o d", o=1)[:, 0:VD])
+            nc.sync.dma_start(out=rows_gb[0:1, VD:2 * VD], in_=ln_b.rearrange("(o d) -> o d", o=1)[:, 0:VD])
+            nc.sync.dma_start(out=gb_rows[0:NJ, :], in_=ln_g.rearrange("(j p) -> j p", p=P))
+            nc.sync.dma_start(out=gb_rows[NJ:2 * NJ, :], in_=ln_b.rearrange("(j p) -> j p", p=P))
             load_r(2)
             load_r(3)
 
@@ -352,18 +354,6 @@ def tile_multiheadattention_pb_kernel(tc, attn_out, residual, proj_w, proj_b, ln
             w_interleave(1, "scalar")
             w_quantise(0)
 
-            for c in range(VD // CH):
-                cs = slice(c * CH, (c + 1) * CH)
-                nc.tensor.matmul(
-                    out=g_ps[:, cs], lhsT=ones_b[:], rhs=rows[:, D + c * CH:D + (c + 1) * CH], start=True, stop=True
-                )
-                nc.tensor.matmul(
-                    out=be_ps[:, cs], lhsT=ones_b[:], rhs=rows[:, D + VD + c * CH:D + VD + (c + 1) * CH],
-                    start=True, stop=True,
-                )
-            gbt = psum.tile([P, P], BF16, name="gbt", tag="t1")
-            nc.tensor.transpose(gbt[:], gb_rows[:], ident_b[:])
-            nc.vector.tensor_copy(out=gb_col[:], in_=gbt[:, 0:2 * NJ])
             pb = []
             for k in range(2):
                 pb.append(psum.tile([P, 2 * CH], BF16, name="pb", tag="t1"))
@@ -429,13 +419,22 @@ def tile_multiheadattention_pb_kernel(tc, attn_out, residual, proj_w, proj_b, ln
         sums_of(1)
         sums_of(2)
 
-        nc.scalar.copy(out=g_bc[:], in_=g_ps[:])
+        for c in range(VD // CH):
+            cs = slice(c * CH, (c + 1) * CH)
+            nc.tensor.matmul(out=g_ps[:, cs], lhsT=ones_b[:], rhs=rows_gb[:, c * CH:(c + 1) * CH], start=True, stop=True)
+            nc.tensor.matmul(
+                out=be_ps[:, cs], lhsT=ones_b[:], rhs=rows_gb[:, VD + c * CH:VD + (c + 1) * CH], start=True, stop=True
+            )
+        gbt = psum.tile([P, P], BF16, name="gbt", tag="t1")
+        nc.tensor.transpose(gbt[:], gb_rows[:], ident_b[:])
+        nc.vector.tensor_copy(out=gb_col[:], in_=gbt[:, 0:2 * NJ])
         mean_of(0)
         squares(0)
         mean_of(1)
         inv_sd(0)
         shift_of(0)
         normalise(0)
+        nc.scalar.copy(out=g_bc[:], in_=g_ps[:])
         nc.scalar.copy(out=be_bc[:], in_=be_ps[:])
         sums_of(3)
         sums_of(4)

@@ -222,8 +222,6 @@ def tile_multiheadattention_pb_kernel(tc, attn_out, residual, proj_w, proj_b, ln
             vd = VDQ[i // 2]
             if (i in GD_TILES) != late:
                 return
-            if late:
-                nc.sync.dma_start(out=o0_view[i][:, 0:vd], in_=o_sb[i][:, 0:vd])
             nc.vector.tensor_reduce(
                 out=am[:, i * NCH:i * NCH + 1], in_=o_sb[i][:, 0:vd], axis=AX.X, op=ALU.max, apply_absolute_value=True
             )
@@ -492,6 +490,9 @@ def tile_multiheadattention_pb_kernel(tc, attn_out, residual, proj_w, proj_b, ln
                 to_features(tail[k], "t1" if k % 2 == 0 else "mm")
             if 0 <= k - 1 < n:
                 gain_bias(tail[k - 1])
+            if k == n:
+                for i in GD_TILES:
+                    nc.sync.dma_start(out=o0_view[i][:, 0:VDQ[i // 2]], in_=o_sb[i][:, 0:VDQ[i // 2]])
             if 0 <= k - 2 < n:
                 copy_out(tail[k - 2])
             if 0 <= k - 1 < n:

@@ -331,9 +331,9 @@ def tile_multiheadattention_pb_kernel(tc, attn_out, residual, proj_w, proj_b, ln
             load_x(1)
             load_w(0)
             load_w(1)
-            nc.sync.dma_start(out=rows[0:1, 0:D], in_=proj_b.rearrange("(o d) -> o d", o=1))
             load_w(2)
             load_w(3)
+            nc.sync.dma_start(out=rows[0:1, 0:D], in_=proj_b.rearrange("(o d) -> o d", o=1))
             load_r(0)
             for i in range(2, NT):
                 load_x(i)
@@ -352,15 +352,6 @@ def tile_multiheadattention_pb_kernel(tc, attn_out, residual, proj_w, proj_b, ln
             w_interleave(1, "scalar")
             w_quantise(0)
 
-            pb = []
-            for k in range(2):
-                pb.append(psum.tile([P, 2 * CH], BF16, name="pb", tag="t1"))
-                for c in range(2):
-                    nc.tensor.matmul(
-                        out=pb[k][:, c * CH:(c + 1) * CH], lhsT=ones_b[:],
-                        rhs=rows[:, (2 * k + c) * CH:(2 * k + c + 1) * CH], start=True, stop=True,
-                    )
-
             w_interleave(2, "vector")
             w_interleave(3, "scalar")
             w_quantise(1)
@@ -372,6 +363,14 @@ def tile_multiheadattention_pb_kernel(tc, attn_out, residual, proj_w, proj_b, ln
             add_residual_chunk(0, 1)
             w_quantise(3)
             add_residual_chunk(0, 2)
+            pb = []
+            for k in range(2):
+                pb.append(psum.tile([P, 2 * CH], BF16, name="pb", tag="t1"))
+                for c in range(2):
+                    nc.tensor.matmul(
+                        out=pb[k][:, c * CH:(c + 1) * CH], lhsT=ones_b[:],
+                        rhs=rows[:, (2 * k + c) * CH:(2 * k + c + 1) * CH], start=True, stop=True,
+                    )
             for a in range(1, NT // 2):
                 x_transpose(a)
                 x_copy(a)

@@ -377,7 +377,8 @@ def tile_multiheadattention_pb_kernel(tc, attn_out, residual, proj_w, proj_b, ln
             project_chunk(0, 3)
             x_quantise(1, 1)
             add_residual_chunk(0, 3)
-            x_quantise(2, 2)
+            x_quantise(2, 1)
+            x_quantise(3, 1)
             for k in range(2):
                 nc.scalar.copy(out=b_bc[:, 2 * k * CH:2 * (k + 1) * CH], in_=pb[k][:])
 
@@ -424,13 +425,13 @@ def tile_multiheadattention_pb_kernel(tc, attn_out, residual, proj_w, proj_b, ln
             )
         gbt = psum.tile([P, P], BF16, name="gbt", tag="t1")
         nc.tensor.transpose(gbt[:], gb_rows[:], ident_b[:])
-        nc.vector.tensor_copy(out=gb_col[:], in_=gbt[:, 0:2 * NJ])
         mean_of(0)
         squares(0)
         mean_of(1)
         inv_sd(0)
         shift_of(0)
         normalise(0)
+        nc.scalar.copy(out=gb_col[:], in_=gbt[:, 0:2 * NJ])
         nc.scalar.copy(out=g_bc[:], in_=g_ps[:])
         nc.scalar.copy(out=be_bc[:], in_=be_ps[:])
         sums_of(3)

@@ -432,8 +432,6 @@ def tile_multiheadattention_pb_kernel(tc, attn_out, residual, proj_w, proj_b, ln
         shift_of(0)
         normalise(0)
         nc.scalar.copy(out=gb_col[:], in_=gbt[:, 0:2 * NJ])
-        nc.scalar.copy(out=g_bc[:], in_=g_ps[:])
-        nc.scalar.copy(out=be_bc[:], in_=be_ps[:])
         sums_of(3)
         sums_of(4)
 
@@ -445,6 +443,8 @@ def tile_multiheadattention_pb_kernel(tc, attn_out, residual, proj_w, proj_b, ln
         sums_of(5)
         sums_of(6)
         sums_of(7)
+        nc.sync.dma_start(out=g_bc[:], in_=ln_g[0:VD].partition_broadcast(P))
+        nc.sync.dma_start(out=be_bc[:], in_=ln_b[0:VD].partition_broadcast(P))
         to_features(early[0], "t1")
 
         squares(2)

@@ -30,7 +30,8 @@ NJ = D // P
 VD = 1024
 VDQ = (1024, 1024, 1024, 1024)
 R_BUFS = 4
-GD_TILES = (7,)
+GD_FROM = {5: 512, 7: 0}
+PE_TILE = 3
 G_NORM = 4
 
 
@@ -72,15 +73,20 @@ def tile_multiheadattention_pb_kernel(tc, attn_out, residual, proj_w, proj_b, ln
         am = keep.tile([P, NT * NCH], F32, name="am")
         g_bc = keep.tile([P, VD], BF16, name="g_bc")
         be_bc = keep.tile([P, VD], BF16, name="be_bc")
-        bsum = keep.tile([P, 1], F32, name="bsum")
+        bc_rows = keep.tile([P, P], BF16, name="bc_rows")
+        b_colf = keep.tile([P, NJ], F32, name="b_colf")
+        bpart = keep.tile([P, 2], F32, name="bpart")
+        ones_f = keep.tile([P, P], F32, name="ones_f")
         nbq = keep.tile([P, 1], F32, name="nbq")
         gb_col = keep.tile([P, 2 * NJ], F32, name="gb_col")
         xg = keep.tile([P, NT * P * 4], BF16, name="xg", align_bytes=64)
         x_codes = keep.tile([P, NT * P], U32, name="x_codes", align_bytes=64)
         x_scales = keep.tile([P, NT * P], U8, name="x_scales", align_bytes=64)
         rows_gb = keep.tile([P, 2 * VD], BF16, name="rows_gb")
-        g_ps = cpsum.tile([P, VD], BF16, name="g_ps")
-        be_ps = cpsum.tile([P, VD], BF16, name="be_ps")
+        bct = cpsum.tile([P, VD], BF16, name="bct", tag="g_ps")
+        bs_ps = cpsum.tile([P, 2], F32, name="bs_ps", tag="be_ps")
+        spread = {}
+        rb_ps = {}
 
         r_sb = {}
         y_sb = {}
@@ -121,7 +127,7 @@ def tile_multiheadattention_pb_kernel(tc, attn_out, residual, proj_w, proj_b, ln
             )
 
         def project_chunk(i, c):
-            if c == 0:
+            if i not in y_sb:
                 y_sb[i] = work.tile([P, D], F32, name="y", tag="y")
             acc = psum.tile([P, CH], F32, name="acc", tag="mm", bufs=4)
             nc.tensor.matmul_mx(
@@ -138,7 +144,8 @@ def tile_multiheadattention_pb_kernel(tc, attn_out, residual, proj_w, proj_b, ln
         def add_residual_chunk(i, c):
             cs = slice(c * CH, (c + 1) * CH)
             nc.vector.scalar_tensor_tensor(
-                out=y_sb[i][:, cs], in0=acc_ps[(i, c)][:], scalar=1.0, in1=r_sb[i][:, cs], op0=ALU.mult, op1=ALU.add,
+                out=y_sb[i][:, cs], in0=acc_ps[(i, c)][:], scalar=1.0,
+                in1=y_sb[i][:, cs] if i == PE_TILE else r_sb[i][:, cs], op0=ALU.mult, op1=ALU.add,
                 accum_out=sums[:, i, c:c + 1],
             )
 
@@ -147,7 +154,23 @@ def tile_multiheadattention_pb_kernel(tc, attn_out, residual, proj_w, proj_b, ln
                 project_chunk(i, c)
                 add_residual_chunk(i, c)
 
+        def rb_sum(i, c):
+            rb = psum.tile([P, CH], F32, name="rb", tag="t1")
+            nc.tensor.matmul(out=rb[:], lhsT=ident_b[:], rhs=r_sb[i][:, c * CH:(c + 1) * CH], start=True, stop=False)
+            for k in range(CH // P):
+                j = c * (CH // P) + k
+                nc.tensor.matmul(
+                    out=rb[:, k * P:(k + 1) * P], lhsT=b_colf[:, j:j + 1].to_broadcast([P, P]), rhs=ident[:],
+                    is_transpose=True, start=False, stop=(k == CH // P - 1),
+                )
+            rb_ps[c] = rb
+
+        def rb_copy(i, c):
+            nc.scalar.copy(out=y_sb[i][:, c * CH:(c + 1) * CH], in_=rb_ps[c][:])
+
         def add_bias(i, pieces):
+            if i == PE_TILE:
+                return
             w = D // pieces
             for k in range(pieces):
                 ks = slice(k * w, (k + 1) * w)
@@ -155,7 +178,8 @@ def tile_multiheadattention_pb_kernel(tc, attn_out, residual, proj_w, proj_b, ln
 
         def mean_of(i):
             nc.scalar.activation(
-                out=sums_s[:, i, :], in_=sums[:, i, :], func=ACT.Identity, scale=-1.0 / D, bias=nbq[:, 0:1],
+                out=sums_s[:, i, :], in_=sums[:, i, :], func=ACT.Identity, scale=-1.0 / D,
+                bias=0.0 if i == PE_TILE else nbq[:, 0:1],
                 accum_out=negmu[:, i:i + 1],
             )
 
@@ -191,40 +215,50 @@ def tile_multiheadattention_pb_kernel(tc, attn_out, residual, proj_w, proj_b, ln
 
         def gpsimd_direct(i):
             ic = slice(i, i + 1)
-            vd = VDQ[i // 2]
+            gs = slice(GD_FROM[i], VDQ[i // 2])
             nc.gpsimd.tensor_scalar(
-                out=y_sb[i][:, 0:vd], in0=y_sb[i][:, 0:vd], scalar1=negmu[:, ic], scalar2=rstd[:, ic],
+                out=y_sb[i][:, gs], in0=y_sb[i][:, gs], scalar1=negmu[:, ic], scalar2=rstd[:, ic],
                 op0=ALU.add, op1=ALU.mult,
             )
-            nc.gpsimd.tensor_tensor(out=y_sb[i][:, 0:vd], in0=y_sb[i][:, 0:vd], in1=g_bc[:, 0:vd], op=ALU.mult)
-            nc.gpsimd.tensor_tensor(out=o_sb[i][:, 0:vd], in0=y_sb[i][:, 0:vd], in1=be_bc[:, 0:vd], op=ALU.add)
+            nc.gpsimd.tensor_tensor(out=y_sb[i][:, gs], in0=y_sb[i][:, gs], in1=g_bc[:, gs], op=ALU.mult)
+            nc.gpsimd.tensor_tensor(out=o_sb[i][:, gs], in0=y_sb[i][:, gs], in1=be_bc[:, gs], op=ALU.add)
 
         def direct_gain(i):
-            vd = VDQ[i // 2]
-            if i in GD_TILES:
+            vd = GD_FROM.get(i, VDQ[i // 2])
+            if vd == 0:
                 return
             nc.vector.scalar_tensor_tensor(
-                out=y_sb[i][:, 0:vd], in0=y_sb[i][:, 0:vd], scalar=negmu[:, i:i + 1], in1=g_ps[:, 0:vd], op0=ALU.add,
+                out=y_sb[i][:, 0:vd], in0=y_sb[i][:, 0:vd], scalar=negmu[:, i:i + 1], in1=spread["g"][:, 0:vd], op0=ALU.add,
                 op1=ALU.mult,
             )
 
         def direct_bias(i):
-            vd = VDQ[i // 2]
-            if i in GD_TILES:
+            vd = GD_FROM.get(i, VDQ[i // 2])
+            if vd == 0:
                 return
             nc.vector.scalar_tensor_tensor(
-                out=o_sb[i][:, 0:vd], in0=y_sb[i][:, 0:vd], scalar=rstd[:, i:i + 1], in1=be_ps[:, 0:vd], op0=ALU.mult,
+                out=o_sb[i][:, 0:vd], in0=y_sb[i][:, 0:vd], scalar=rstd[:, i:i + 1], in1=spread["be"][:, 0:vd], op0=ALU.mult,
                 op1=ALU.add,
             )
             nc.sync.dma_start(out=o0_view[i][:, 0:vd], in_=o_sb[i][:, 0:vd])
 
-        def direct_absmax(i, late=False):
-            vd = VDQ[i // 2]
-            if (i in GD_TILES) != late:
+        def direct_absmax(i):
+            vd = GD_FROM.get(i, VDQ[i // 2])
+            if vd == 0:
                 return
             nc.vector.tensor_reduce(
                 out=am[:, i * NCH:i * NCH + 1], in_=o_sb[i][:, 0:vd], axis=AX.X, op=ALU.max, apply_absolute_value=True
             )
+
+        def gpsimd_absmax(i):
+            nc.vector.tensor_reduce(
+                out=am[:, i * NCH + 1:i * NCH + 2], in_=o_sb[i][:, GD_FROM[i]:VDQ[i // 2]], axis=AX.X, op=ALU.max,
+                apply_absolute_value=True,
+            )
+
+        def gpsimd_store(i):
+            gs = slice(GD_FROM[i], VDQ[i // 2])
+            nc.sync.dma_start(out=o0_view[i][:, gs], in_=o_sb[i][:, gs])
 
         def to_features(u, tag):
             q, c = u
@@ -320,6 +354,9 @@ def tile_multiheadattention_pb_kernel(tc, attn_out, residual, proj_w, proj_b, ln
             nc.vector.memset(rows_gb[:].bitcast(F32), 0.0)
             nc.vector.memset(ones_b[:], 1.0)
             nc.vector.memset(gb_rows[:], 0.0)
+            nc.vector.memset(bc_rows[:], 0.0)
+            nc.vector.memset(ones_f[:], 1.0)
+            nc.vector.memset(bpart[:], 0.0)
             nc.vector.memset(ones[:], 1.0)
             nc.vector.memset(zeros[:], 0.0)
             nc.vector.memset(am[:], 0.0)
@@ -335,6 +372,7 @@ def tile_multiheadattention_pb_kernel(tc, attn_out, residual, proj_w, proj_b, ln
             load_w(3)
             nc.sync.dma_start(out=rows[0:1, 0:D], in_=proj_b.rearrange("(o d) -> o d", o=1))
             load_r(0)
+            nc.sync.dma_start(out=bc_rows[0:NJ, :], in_=proj_b.rearrange("(j p) -> j p", p=P))
             for i in range(2, NT):
                 load_x(i)
             load_r(1)
@@ -371,6 +409,7 @@ def tile_multiheadattention_pb_kernel(tc, attn_out, residual, proj_w, proj_b, ln
                         out=pb[k][:, c * CH:(c + 1) * CH], lhsT=ones_b[:],
                         rhs=rows[:, (2 * k + c) * CH:(2 * k + c + 1) * CH], start=True, stop=True,
                     )
+            nc.tensor.transpose(bct[:, 0:P], bc_rows[:], ident_b[:])
             for a in range(1, NT // 2):
                 x_transpose(a)
                 x_copy(a)
@@ -379,6 +418,7 @@ def tile_multiheadattention_pb_kernel(tc, attn_out, residual, proj_w, proj_b, ln
             add_residual_chunk(0, 3)
             x_quantise(2, 1)
             x_quantise(3, 1)
+            nc.scalar.activation(out=b_colf[:], in_=bct[:, 0:NJ], func=ACT.Copy, accum_out=bpart[:, 0:1])
             for k in range(2):
                 nc.scalar.copy(out=b_bc[:, 2 * k * CH:2 * (k + 1) * CH], in_=pb[k][:])
 
@@ -411,11 +451,28 @@ def tile_multiheadattention_pb_kernel(tc, attn_out, residual, proj_w, proj_b, ln
 
         add_bias(0, 2)
         load_r(R_BUFS)
-        b_junk = late.tile([P, D], BF16, name="b_junk", tag="sq")
-        nc.scalar.activation(out=b_junk[:], in_=b_bc[:], func=ACT.Copy, accum_out=bsum[:, 0:1])
-        nc.scalar.activation(out=nbq[:], in_=bsum[:, 0:1], func=ACT.Copy, scale=-1.0 / (NCH * D))
+        nc.tensor.matmul(out=bs_ps[:], lhsT=ones_f[:], rhs=bpart[:], start=True, stop=True)
+        nc.scalar.activation(out=nbq[:], in_=bs_ps[:, 0:1], func=ACT.Copy, scale=-1.0 / (NCH * D))
         sums_of(1)
-        sums_of(2)
+        y_sb[PE_TILE] = work.tile([P, D], F32, name="y", tag="y")
+        for c in range(NCH):
+            rb_sum(PE_TILE, c)
+            rb_copy(PE_TILE, c)
+            project_chunk(2, c)
+            add_residual_chunk(2, c)
+        add_bias(2, 1)
+        load_r(2 + R_BUFS)
+        mean_of(0)
+        squares(0)
+        mean_of(1)
+        inv_sd(0)
+        shift_of(0)
+        normalise(0)
+        sums_of(3)
+        spread["g"] = cpsum.tile([P, VD], BF16, name="g_ps", tag="g_ps")
+        spread["be"] = cpsum.tile([P, VD], BF16, name="be_ps", tag="be_ps")
+        g_ps = spread["g"]
+        be_ps = spread["be"]
 
         for c in range(VD // CH):
             cs = slice(c * CH, (c + 1) * CH)
@@ -425,18 +482,15 @@ def tile_multiheadattention_pb_kernel(tc, attn_out, residual, proj_w, proj_b, ln
             )
         gbt = psum.tile([P, P], BF16, name="gbt", tag="t1")
         nc.tensor.transpose(gbt[:], gb_rows[:], ident_b[:])
-        mean_of(0)
-        squares(0)
-        mean_of(1)
-        inv_sd(0)
-        shift_of(0)
-        normalise(0)
-        nc.scalar.copy(out=gb_col[:], in_=gbt[:, 0:2 * NJ])
-        sums_of(3)
         sums_of(4)
+        mean_of(3)
+        nc.scalar.copy(out=gb_col[:], in_=gbt[:, 0:2 * NJ])
+        squares(3)
+        mean_of(2)
+        inv_sd(3)
 
         squares(1)
-        mean_of(2)
+        shift_of(3)
         inv_sd(1)
         shift_of(1)
         normalise(1)
@@ -452,13 +506,12 @@ def tile_multiheadattention_pb_kernel(tc, attn_out, residual, proj_w, proj_b, ln
         to_tokens(early[0])
         to_features(early[1], "t1")
         normalise(2)
-        copy_out(early[0], ((mean_of, 3),))
+        copy_out(early[0])
 
         direct_step(0)
         direct_step(1)
         direct_step(2)
-        squares(3)
-        gain_bias(early[1], ((inv_sd, 3), (shift_of, 3)))
+        gain_bias(early[1])
         to_tokens(early[1])
         normalise(3)
         to_features(early[2], "t1")
@@ -472,6 +525,7 @@ def tile_multiheadattention_pb_kernel(tc, attn_out, residual, proj_w, proj_b, ln
         direct_step(4)
         squares(5)
         copy_out(early[2], ((inv_sd, 5),))
+        gpsimd_direct(5)
         mean_of(6)
         gain_bias(early[3], ((mean_of, 7),))
         to_tokens(early[3])
@@ -481,8 +535,7 @@ def tile_multiheadattention_pb_kernel(tc, attn_out, residual, proj_w, proj_b, ln
         direct_step(6)
         squares(7)
         inv_sd(7)
-        for i in GD_TILES:
-            gpsimd_direct(i)
+        gpsimd_direct(7)
 
         n = len(tail)
         for k in range(n + 2):
@@ -491,18 +544,19 @@ def tile_multiheadattention_pb_kernel(tc, attn_out, residual, proj_w, proj_b, ln
             if 0 <= k - 1 < n:
                 gain_bias(tail[k - 1])
             if k == n:
-                for i in GD_TILES:
-                    nc.sync.dma_start(out=o0_view[i][:, 0:VDQ[i // 2]], in_=o_sb[i][:, 0:VDQ[i // 2]])
+                gpsimd_store(5)
+                gpsimd_store(7)
             if 0 <= k - 2 < n:
                 copy_out(tail[k - 2])
             if 0 <= k - 1 < n:
                 to_tokens(tail[k - 1])
             if k < 3:
                 direct_step(NT - 1 + k)
+            if k == 3:
+                gpsimd_absmax(5)
             if 0 <= k - 1 < n:
                 unit_absmax_early(tail[k - 1])
-        for i in GD_TILES:
-            direct_absmax(i, True)
+        gpsimd_absmax(7)
 
         pm = keep.tile([P, 1], F32, name="pm")
         am_s = keep.tile([P, NT * NCH], F32, name="am_s")

@@ -82,7 +82,8 @@ def tile_multiheadattention_pb_kernel(tc, attn_out, residual, proj_w, proj_b, ln
         xg = keep.tile([P, NT * P * 4], BF16, name="xg", align_bytes=64)
         x_codes = keep.tile([P, NT * P], U32, name="x_codes", align_bytes=64)
         x_scales = keep.tile([P, NT * P], U8, name="x_scales", align_bytes=64)
-        rows_gb = keep.tile([P, 2 * VD], BF16, name="rows_gb")
+        rows = keep.tile([P, D], BF16, name="rows")
+        gb_colb = keep.tile([P, 2 * NJ], BF16, name="gb_colb")
         bct = cpsum.tile([P, VD], BF16, name="bct", tag="g_ps")
         bs_ps = cpsum.tile([P, 2], F32, name="bs_ps", tag="be_ps")
         spread = {}
@@ -157,12 +158,7 @@ def tile_multiheadattention_pb_kernel(tc, attn_out, residual, proj_w, proj_b, ln
         def rb_sum(i, c):
             rb = psum.tile([P, CH], F32, name="rb", tag="t1")
             nc.tensor.matmul(out=rb[:], lhsT=ident_b[:], rhs=r_sb[i][:, c * CH:(c + 1) * CH], start=True, stop=False)
-            for k in range(CH // P):
-                j = c * (CH // P) + k
-                nc.tensor.matmul(
-                    out=rb[:, k * P:(k + 1) * P], lhsT=b_colf[:, j:j + 1].to_broadcast([P, P]), rhs=ident[:],
-                    is_transpose=True, start=False, stop=(k == CH // P - 1),
-                )
+            nc.tensor.matmul(out=rb[:], lhsT=ones_b[:], rhs=rows[:, c * CH:(c + 1) * CH], start=False, stop=True)
             rb_ps[c] = rb
 
         def rb_copy(i, c):
@@ -333,7 +329,6 @@ def tile_multiheadattention_pb_kernel(tc, attn_out, residual, proj_w, proj_b, ln
                 wg.append(wpool.tile([P, CH, 4], BF16, name="wg%d" % c, align_bytes=64))
                 w_codes.append(keep.tile([P, CH], U32, name="w_codes%d" % c, align_bytes=64))
                 w_scales.append(keep.tile([P, CH], U8, name="w_scales%d" % c, align_bytes=64))
-            rows = wpool.tile([P, D], BF16, name="rows")
 
             def load_w(c):
                 nc.sync.dma_start(out=w_raw[c][:], in_=w_view[:, :, c * CH:(c + 1) * CH])
@@ -351,7 +346,6 @@ def tile_multiheadattention_pb_kernel(tc, attn_out, residual, proj_w, proj_b, ln
                 )
 
             nc.vector.memset(rows[:].bitcast(F32), 0.0)
-            nc.vector.memset(rows_gb[:].bitcast(F32), 0.0)
             nc.vector.memset(ones_b[:], 1.0)
             nc.vector.memset(gb_rows[:], 0.0)
             nc.vector.memset(bc_rows[:], 0.0)
@@ -376,8 +370,6 @@ def tile_multiheadattention_pb_kernel(tc, attn_out, residual, proj_w, proj_b, ln
             for i in range(2, NT):
                 load_x(i)
             load_r(1)
-            nc.sync.dma_start(out=rows_gb[0:1, 0:VD], in_=ln_g.rearrange("(o d) -> o d", o=1)[:, 0:VD])
-            nc.sync.dma_start(out=rows_gb[0:1, VD:2 * VD], in_=ln_b.rearrange("(o d) -> o d", o=1)[:, 0:VD])
             nc.sync.dma_start(out=gb_rows[0:NJ, :], in_=ln_g.rearrange("(j p) -> j p", p=P))
             nc.sync.dma_start(out=gb_rows[NJ:2 * NJ, :], in_=ln_b.rearrange("(j p) -> j p", p=P))
             load_r(2)
@@ -469,22 +461,12 @@ def tile_multiheadattention_pb_kernel(tc, attn_out, residual, proj_w, proj_b, ln
         shift_of(0)
         normalise(0)
         sums_of(3)
-        spread["g"] = cpsum.tile([P, VD], BF16, name="g_ps", tag="g_ps")
-        spread["be"] = cpsum.tile([P, VD], BF16, name="be_ps", tag="be_ps")
-        g_ps = spread["g"]
-        be_ps = spread["be"]
-
-        for c in range(VD // CH):
-            cs = slice(c * CH, (c + 1) * CH)
-            nc.tensor.matmul(out=g_ps[:, cs], lhsT=ones_b[:], rhs=rows_gb[:, c * CH:(c + 1) * CH], start=True, stop=True)
-            nc.tensor.matmul(
-                out=be_ps[:, cs], lhsT=ones_b[:], rhs=rows_gb[:, VD + c * CH:VD + (c + 1) * CH], start=True, stop=True
-            )
         gbt = psum.tile([P, P], BF16, name="gbt", tag="t1")
         nc.tensor.transpose(gbt[:], gb_rows[:], ident_b[:])
         sums_of(4)
         mean_of(3)
         nc.scalar.copy(out=gb_col[:], in_=gbt[:, 0:2 * NJ])
+        nc.scalar.copy(out=gb_colb[:], in_=gbt[:, 0:2 * NJ])
         squares(3)
         mean_of(2)
         inv_sd(3)
@@ -495,6 +477,14 @@ def tile_multiheadattention_pb_kernel(tc, attn_out, residual, proj_w, proj_b, ln
         shift_of(1)
         normalise(1)
         sums_of(5)
+        spread["g"] = cpsum.tile([P, VD], BF16, name="g_ps", tag="g_ps")
+        spread["be"] = cpsum.tile([P, VD], BF16, name="be_ps", tag="be_ps")
+        for j in range(VD // P):
+            nc.tensor.transpose(spread["g"][:, j * P:(j + 1) * P], gb_colb[:, j:j + 1].to_broadcast([P, P]), ident_b[:])
+        for j in range(VD // P):
+            nc.tensor.transpose(
+                spread["be"][:, j * P:(j + 1) * P], gb_colb[:, NJ + j:NJ + j + 1].to_broadcast([P, P]), ident_b[:]
+            )
         sums_of(6)
         sums_of(7)
         nc.sync.dma_start(out=g_bc[:], in_=ln_g[0:VD].partition_broadcast(P))

@@ -372,8 +372,8 @@ def tile_multiheadattention_pb_kernel(tc, attn_out, residual, proj_w, proj_b, ln
             load_r(1)
             nc.sync.dma_start(out=gb_rows[0:NJ, :], in_=ln_g.rearrange("(j p) -> j p", p=P))
             nc.sync.dma_start(out=gb_rows[NJ:2 * NJ, :], in_=ln_b.rearrange("(j p) -> j p", p=P))
-            load_r(2)
             load_r(3)
+            load_r(2)
 
             x_transpose(0)
             x_copy(0)
@@ -448,10 +448,10 @@ def tile_multiheadattention_pb_kernel(tc, attn_out, residual, proj_w, proj_b, ln
         sums_of(1)
         y_sb[PE_TILE] = work.tile([P, D], F32, name="y", tag="y")
         for c in range(NCH):
-            rb_sum(PE_TILE, c)
-            rb_copy(PE_TILE, c)
             project_chunk(2, c)
             add_residual_chunk(2, c)
+            rb_sum(PE_TILE, c)
+            rb_copy(PE_TILE, c)
         add_bias(2, 1)
         load_r(2 + R_BUFS)
         mean_of(0)

@@ -30,8 +30,9 @@ NJ = D // P
 VD = 1024
 VDQ = (1024, 1024, 1024, 1024)
 R_BUFS = 4
-GD_FROM = {5: 512, 7: 0}
+GD_FROM = {5: 256, 7: 0}
 PE_TILE = 3
+GN_TILES = (5, 6, 7)
 G_NORM = 4
 
 
@@ -68,6 +69,8 @@ def tile_multiheadattention_pb_kernel(tc, attn_out, residual, proj_w, proj_b, ln
         sums_s = keep.tile([P, NT, NCH], F32, name="sums_s")
         negmu = keep.tile([P, NT], F32, name="negmu")
         ssq = keep.tile([P, NT], F32, name="ssq")
+        ssq_h = keep.tile([P, 2], F32, name="ssq_h")
+        ssq_j = keep.tile([P, 2], F32, name="ssq_j")
         rstd = keep.tile([P, NT], F32, name="rstd")
         nmr = keep.tile([P, NT], F32, name="nmr")
         am = keep.tile([P, NT * NCH], F32, name="am")
@@ -186,12 +189,23 @@ def tile_multiheadattention_pb_kernel(tc, attn_out, residual, proj_w, proj_b, ln
                 accum_out=ssq[:, i:i + 1],
             )
 
+        def squares_half(i, h):
+            sq = late.tile([P, D], BF16, name="sq", tag="sq")
+            hs = slice(h * (D // 2), (h + 1) * (D // 2))
+            nc.scalar.activation(
+                out=sq[:, hs], in_=y_sb[i][:, hs], func=ACT.Square, bias=negmu[:, i:i + 1], scale=1.0,
+                accum_out=ssq_h[:, h:h + 1],
+            )
+
+        def squares_join(i):
+            nc.scalar.activation(out=ssq_j[:], in_=ssq_h[:], func=ACT.Copy, accum_out=ssq[:, i:i + 1])
+
         def inv_sd(i):
             ic = slice(i, i + 1)
             nc.scalar.activation(
                 out=rstd[:, ic], in_=ssq[:, ic], func=ACT.Abs_reciprocal_sqrt, bias=LN_EPS, scale=1.0 / D
             )
-            if i >= G_NORM:
+            if i in GN_TILES:
                 vd = VDQ[i // 2]
                 nc.gpsimd.tensor_scalar(
                     out=y_sb[i][:, vd:D], in0=y_sb[i][:, vd:D], scalar1=negmu[:, ic], scalar2=rstd[:, ic],
@@ -452,11 +466,16 @@ def tile_multiheadattention_pb_kernel(tc, attn_out, residual, proj_w, proj_b, ln
             add_residual_chunk(2, c)
             rb_sum(PE_TILE, c)
             rb_copy(PE_TILE, c)
+            if c == 0:
+                mean_of(0)
+            if c == 1:
+                squares_half(0, 0)
         add_bias(2, 1)
         load_r(2 + R_BUFS)
-        mean_of(0)
-        squares(0)
+        squares_half(0, 1)
         mean_of(1)
+        squares_join(0)
+        mean_of(2)
         inv_sd(0)
         shift_of(0)
         normalise(0)
@@ -468,12 +487,10 @@ def tile_multiheadattention_pb_kernel(tc, attn_out, residual, proj_w, proj_b, ln
         nc.scalar.copy(out=gb_col[:], in_=gbt[:, 0:2 * NJ])
         nc.scalar.copy(out=gb_colb[:], in_=gbt[:, 0:2 * NJ])
         squares(3)
-        mean_of(2)
-        inv_sd(3)
-
         squares(1)
-        shift_of(3)
+        inv_sd(3)
         inv_sd(1)
+        shift_of(3)
         shift_of(1)
         normalise(1)
         sums_of(5)
@@ -508,8 +525,9 @@ def tile_multiheadattention_pb_kernel(tc, attn_out, residual, proj_w, proj_b, ln
         copy_out(early[1], ((mean_of, 4),))
 
         squares(4)
-        gain_bias(early[2], ((inv_sd, 4), (mean_of, 5)))
+        gain_bias(early[2], ((inv_sd, 4), (mean_of, 5), (shift_of, 4)))
         to_tokens(early[2])
+        normalise(4)
         to_features(early[3], "t1")
         direct_step(3)
         direct_step(4)

@@ -25,7 +25,7 @@ NCH = D // CH
 LN_EPS = 1e-5
 FLOPS = 2 * LQ * K * D
 
-CAST_V = 1344
+CAST_V = 1376
 NJ = D // P
 VD = 1024
 VDQ = (1024, 1024, 1024, 1024)
@@ -206,7 +206,7 @@ def tile_multiheadattention_pb_kernel(tc, attn_out, residual, proj_w, proj_b, ln
                 out=rstd[:, ic], in_=ssq[:, ic], func=ACT.Abs_reciprocal_sqrt, bias=LN_EPS, scale=1.0 / D
             )
             if i in GN_TILES:
-                vd = VDQ[i // 2]
+                vd = GD_FROM.get(i, VDQ[i // 2])
                 nc.gpsimd.tensor_scalar(
                     out=y_sb[i][:, vd:D], in0=y_sb[i][:, vd:D], scalar1=negmu[:, ic], scalar2=rstd[:, ic],
                     op0=ALU.add, op1=ALU.mult,
@@ -226,10 +226,11 @@ def tile_multiheadattention_pb_kernel(tc, attn_out, residual, proj_w, proj_b, ln
         def gpsimd_direct(i):
             ic = slice(i, i + 1)
             gs = slice(GD_FROM[i], VDQ[i // 2])
-            nc.gpsimd.tensor_scalar(
-                out=y_sb[i][:, gs], in0=y_sb[i][:, gs], scalar1=negmu[:, ic], scalar2=rstd[:, ic],
-                op0=ALU.add, op1=ALU.mult,
-            )
+            if i not in GN_TILES:
+                nc.gpsimd.tensor_scalar(
+                    out=y_sb[i][:, gs], in0=y_sb[i][:, gs], scalar1=negmu[:, ic], scalar2=rstd[:, ic],
+                    op0=ALU.add, op1=ALU.mult,
+                )
             nc.gpsimd.tensor_tensor(out=y_sb[i][:, gs], in0=y_sb[i][:, gs], in1=g_bc[:, gs], op=ALU.mult)
             nc.gpsimd.tensor_tensor(out=o_sb[i][:, gs], in0=y_sb[i][:, gs], in1=be_bc[:, gs], op=ALU.add)
 
@@ -449,7 +450,7 @@ def tile_multiheadattention_pb_kernel(tc, attn_out, residual, proj_w, proj_b, ln
             if 0 <= k - 1 < NT:
                 direct_bias(k - 1)
             if 0 <= k - 3 < len(early):
-                unit_absmax(early[k - 3])
+                unit_absmax_early(early[k - 3])
             if 3 <= k < NT:
                 direct_gain(k)
             if 0 <= k - 2 < NT:
@@ -461,14 +462,16 @@ def tile_multiheadattention_pb_kernel(tc, attn_out, residual, proj_w, proj_b, ln
         nc.scalar.activation(out=nbq[:], in_=bs_ps[:, 0:1], func=ACT.Copy, scale=-1.0 / (NCH * D))
         sums_of(1)
         y_sb[PE_TILE] = work.tile([P, D], F32, name="y", tag="y")
+        rb_sum(PE_TILE, 0)
+        rb_copy(PE_TILE, 0)
+        mean_of(0)
         for c in range(NCH):
             project_chunk(2, c)
             add_residual_chunk(2, c)
-            rb_sum(PE_TILE, c)
-            rb_copy(PE_TILE, c)
+            if c + 1 < NCH:
+                rb_sum(PE_TILE, c + 1)
+                rb_copy(PE_TILE, c + 1)
             if c == 0:
-                mean_of(0)
-            if c == 1:
                 squares_half(0, 0)
         add_bias(2, 1)
         load_r(2 + R_BUFS)
@@ -549,10 +552,11 @@ def tile_multiheadattention_pb_kernel(tc, attn_out, residual, proj_w, proj_b, ln
         for k in range(n + 2):
             if k < n:
                 to_features(tail[k], "t1" if k % 2 == 0 else "mm")
+            if k == 1:
+                gpsimd_store(5)
             if 0 <= k - 1 < n:
                 gain_bias(tail[k - 1])
             if k == n:
-                gpsimd_store(5)
                 gpsimd_store(7)
             if 0 <= k - 2 < n:
                 copy_out(tail[k - 2])

@@ -450,7 +450,7 @@ def tile_multiheadattention_pb_kernel(tc, attn_out, residual, proj_w, proj_b, ln
             if 0 <= k - 1 < NT:
                 direct_bias(k - 1)
             if 0 <= k - 3 < len(early):
-                unit_absmax_early(early[k - 3])
+                unit_absmax(early[k - 3])
             if 3 <= k < NT:
                 direct_gain(k)
             if 0 <= k - 2 < NT:

@@ -45,11 +45,11 @@ def tile_multiheadattention_pb_kernel(tc, attn_out, residual, proj_w, proj_b, ln
         psum = ctx.enter_context(tc.psum_pool(name="psum", bufs=2))
         cpsum = ctx.enter_context(tc.psum_pool(name="cpsum", bufs=1))
 
-        x_view = attn_out.rearrange("h (p i) j -> i p h j", i=NT)
+        x_view = attn_out.rearrange("h (i p) j -> i p h j", i=NT)
         w_view = proj_w.rearrange("(p j) w -> p j w", j=4)
-        r_view = residual.rearrange("(p i) d -> i p d", i=NT)
-        o0_view = out_0.rearrange("(p i) d -> i p d", i=NT)
-        o1_view = out_1.rearrange("(p i) d -> i p d", i=NT)
+        r_view = residual.rearrange("(i p) d -> i p d", i=NT)
+        o0_view = out_0.rearrange("(i p) d -> i p d", i=NT)
+        o1_view = out_1.rearrange("(i p) d -> i p d", i=NT)
 
         x_sb = []
         for i in range(NT):

from contextlib import ExitStack

import concourse.mybir as mybir
from concourse.masks import make_identity

F32 = mybir.dt.float32
BF16 = mybir.dt.bfloat16
U32 = mybir.dt.uint32
U8 = mybir.dt.uint8
FP8X4 = mybir.dt.float8_e4m3fn_x4
FP8 = mybir.dt.float8_e4m3fn
ALU = mybir.AluOpType
ACT = mybir.ActivationFunctionType
AX = mybir.AxisListType

P = 128
LQ = 1024
D = 2048
H = 4
DV = 128
K = H * DV
NT = LQ // P
CH = 512
NCH = D // CH
LN_EPS = 1e-5
FLOPS = 2 * LQ * K * D

CAST_V = 1376
NJ = D // P
VD = 1024
VDQ = (1024, 1024, 1024, 1024)
R_BUFS = 4
GD_FROM = {5: 256, 7: 0}
PE_TILE = 3
GN_TILES = (5, 6, 7)
G_NORM = 4


def tile_multiheadattention_pb_kernel(tc, attn_out, residual, proj_w, proj_b, ln_g, ln_b, out_0, out_1):
    nc = tc.nc
    with ExitStack() as ctx:
        ctx.enter_context(tc.manual_schedule())
        keep = ctx.enter_context(tc.tile_pool(name="keep", bufs=1))
        work = ctx.enter_context(tc.tile_pool(name="work", bufs=8))
        psum = ctx.enter_context(tc.psum_pool(name="psum", bufs=2))
        cpsum = ctx.enter_context(tc.psum_pool(name="cpsum", bufs=1))

        x_view = attn_out.rearrange("h (i p) j -> i p h j", i=NT)
        w_view = proj_w.rearrange("(p j) w -> p j w", j=4)
        r_view = residual.rearrange("(i p) d -> i p d", i=NT)
        o0_view = out_0.rearrange("(i p) d -> i p d", i=NT)
        o1_view = out_1.rearrange("(i p) d -> i p d", i=NT)

        x_sb = []
        for i in range(NT):
            x_sb.append(keep.tile([P, H, DV], BF16, name="x_sb%d" % i))
        b_bc = keep.tile([P, D], BF16, name="b_bc")
        gb_rows = keep.tile([P, P], BF16, name="gb_rows")
        o_sb = []
        for i in range(NT):
            o_sb.append(keep.tile([P, D], F32, name="o_sb%d" % i))
        ident = keep.tile([P, P], F32, name="ident")
        ident_b = keep.tile([P, P], BF16, name="ident_b")
        ones_b = keep.tile([P, P], BF16, name="ones_b")
        ones = keep.tile([P, 1], F32, name="ones")
        zeros = keep.tile([P, 1], F32, name="zeros")
        warm = keep.tile([P, 1], F32, name="warm")
        sums = keep.tile([P, NT, NCH], F32, name="sums")
        sums_s = keep.tile([P, NT, NCH], F32, name="sums_s")
        negmu = keep.tile([P, NT], F32, name="negmu")
        ssq = keep.tile([P, NT], F32, name="ssq")
        ssq_h = keep.tile([P, 2], F32, name="ssq_h")
        ssq_j = keep.tile([P, 2], F32, name="ssq_j")
        rstd = keep.tile([P, NT], F32, name="rstd")
        nmr = keep.tile([P, NT], F32, name="nmr")
        am = keep.tile([P, NT * NCH], F32, name="am")
        g_bc = keep.tile([P, VD], BF16, name="g_bc")
        be_bc = keep.tile([P, VD], BF16, name="be_bc")
        bc_rows = keep.tile([P, P], BF16, name="bc_rows")
        b_colf = keep.tile([P, NJ], F32, name="b_colf")
        bpart = keep.tile([P, 2], F32, name="bpart")
        ones_f = keep.tile([P, P], F32, name="ones_f")
        nbq = keep.tile([P, 1], F32, name="nbq")
        gb_col = keep.tile([P, 2 * NJ], F32, name="gb_col")
        xg = keep.tile([P, NT * P * 4], BF16, name="xg", align_bytes=64)
        x_codes = keep.tile([P, NT * P], U32, name="x_codes", align_bytes=64)
        x_scales = keep.tile([P, NT * P], U8, name="x_scales", align_bytes=64)
        rows = keep.tile([P, D], BF16, name="rows")
        gb_colb = keep.tile([P, 2 * NJ], BF16, name="gb_colb")
        bct = cpsum.tile([P, VD], BF16, name="bct", tag="g_ps")
        bs_ps = cpsum.tile([P, 2], F32, name="bs_ps", tag="be_ps")
        spread = {}
        rb_ps = {}

        r_sb = {}
        y_sb = {}
        acc_ps = {}
        xt_ps = {}
        t1_ps = {}
        t2_ps = {}
        ot_sb = {}
        w_codes = []
        w_scales = []

        def load_x(i):
            nc.sync.dma_start(out=x_sb[i][:], in_=x_view[i])

        def load_r(i):
            r_sb[i] = work.tile([P, D], BF16, name="r_sb", tag="r_sb", bufs=R_BUFS)
            nc.sync.dma_start(out=r_sb[i][:], in_=r_view[i])

        def x_transpose(a):
            xt = psum.tile([P, 2, 2, P], F32, name="xt", tag="mm", bufs=4)
            for e in range(2):
                words = x_sb[2 * a + e][:].rearrange("p h j -> p (h j)").bitcast(F32)
                for u in range(2):
                    nc.tensor.transpose(xt[:, e, u, :], words[:, u::2], ident[:])
            xt_ps[a] = xt

        def x_copy(a):
            nc.scalar.copy(
                out=xg[:, a * 1024:(a + 1) * 1024].bitcast(F32).rearrange("p (e r u) -> p e r u", e=2, u=2),
                in_=xt_ps[a][:].rearrange("p e u r -> p e r u"),
            )

        def x_quantise(a, n):
            nc.vector.quantize_mx(
                out=x_codes[:, a * 256:(a + n) * 256].bitcast(FP8X4),
                scales=x_scales[:, a * 256:(a + n) * 256],
                in_=xg[:, a * 1024:(a + n) * 1024],
            )

        def project_chunk(i, c):
            if i not in y_sb:
                y_sb[i] = work.tile([P, D], F32, name="y", tag="y")
            acc = psum.tile([P, CH], F32, name="acc", tag="mm", bufs=4)
            nc.tensor.matmul_mx(
                out=acc[:],
                lhsT=x_codes[:, i * P:(i + 1) * P].bitcast(FP8X4),
                lhsT_scale=x_scales[:, i * P:(i + 1) * P],
                rhs=w_codes[c][:].bitcast(FP8X4),
                rhs_scale=w_scales[c][:],
                start=True,
                stop=True,
            )
            acc_ps[(i, c)] = acc

        def add_residual_chunk(i, c):
            cs = slice(c * CH, (c + 1) * CH)
            nc.vector.scalar_tensor_tensor(
                out=y_sb[i][:, cs], in0=acc_ps[(i, c)][:], scalar=1.0,
                in1=y_sb[i][:, cs] if i == PE_TILE else r_sb[i][:, cs], op0=ALU.mult, op1=ALU.add,
                accum_out=sums[:, i, c:c + 1],
            )

        def project(i):
            for c in range(NCH):
                project_chunk(i, c)
                add_residual_chunk(i, c)

        def rb_sum(i, c):
            rb = psum.tile([P, CH], F32, name="rb", tag="t1")
            nc.tensor.matmul(out=rb[:], lhsT=ident_b[:], rhs=r_sb[i][:, c * CH:(c + 1) * CH], start=True, stop=False)
            nc.tensor.matmul(out=rb[:], lhsT=ones_b[:], rhs=rows[:, c * CH:(c + 1) * CH], start=False, stop=True)
            rb_ps[c] = rb

        def rb_copy(i, c):
            nc.scalar.copy(out=y_sb[i][:, c * CH:(c + 1) * CH], in_=rb_ps[c][:])

        def add_bias(i, pieces):
            if i == PE_TILE:
                return
            w = D // pieces
            for k in range(pieces):
                ks = slice(k * w, (k + 1) * w)
                nc.gpsimd.tensor_tensor(out=y_sb[i][:, ks], in0=y_sb[i][:, ks], in1=b_bc[:, ks], op=ALU.add)

        def mean_of(i):
            nc.scalar.activation(
                out=sums_s[:, i, :], in_=sums[:, i, :], func=ACT.Identity, scale=-1.0 / D,
                bias=0.0 if i == PE_TILE else nbq[:, 0:1],
                accum_out=negmu[:, i:i + 1],
            )

        def squares(i):
            sq = late.tile([P, D], BF16, name="sq", tag="sq")
            nc.scalar.activation(
                out=sq[:], in_=y_sb[i][:], func=ACT.Square, bias=negmu[:, i:i + 1], scale=1.0,
                accum_out=ssq[:, i:i + 1],
            )

        def squares_half(i, h):
            sq = late.tile([P, D], BF16, name="sq", tag="sq")
            hs = slice(h * (D // 2), (h + 1) * (D // 2))
            nc.scalar.activation(
                out=sq[:, hs], in_=y_sb[i][:, hs], func=ACT.Square, bias=negmu[:, i:i + 1], scale=1.0,
                accum_out=ssq_h[:, h:h + 1],
            )

        def squares_join(i):
            nc.scalar.activation(out=ssq_j[:], in_=ssq_h[:], func=ACT.Copy, accum_out=ssq[:, i:i + 1])

        def inv_sd(i):
            ic = slice(i, i + 1)
            nc.scalar.activation(
                out=rstd[:, ic], in_=ssq[:, ic], func=ACT.Abs_reciprocal_sqrt, bias=LN_EPS, scale=1.0 / D
            )
            if i in GN_TILES:
                vd = GD_FROM.get(i, VDQ[i // 2])
                nc.gpsimd.tensor_scalar(
                    out=y_sb[i][:, vd:D], in0=y_sb[i][:, vd:D], scalar1=negmu[:, ic], scalar2=rstd[:, ic],
                    op0=ALU.add, op1=ALU.mult,
                )

        def shift_of(i):
            ic = slice(i, i + 1)
            nc.scalar.activation(out=nmr[:, ic], in_=negmu[:, ic], func=ACT.Copy, scale=rstd[:, ic])

        def normalise(i):
            ic = slice(i, i + 1)
            vd = VDQ[i // 2]
            nc.scalar.activation(
                out=y_sb[i][:, vd:D], in_=y_sb[i][:, vd:D], func=ACT.Identity, scale=rstd[:, ic], bias=nmr[:, ic]
            )

        def gpsimd_direct(i):
            ic = slice(i, i + 1)
            gs = slice(GD_FROM[i], VDQ[i // 2])
            if i not in GN_TILES:
                nc.gpsimd.tensor_scalar(
                    out=y_sb[i][:, gs], in0=y_sb[i][:, gs], scalar1=negmu[:, ic], scalar2=rstd[:, ic],
                    op0=ALU.add, op1=ALU.mult,
                )
            nc.gpsimd.tensor_tensor(out=y_sb[i][:, gs], in0=y_sb[i][:, gs], in1=g_bc[:, gs], op=ALU.mult)
            nc.gpsimd.tensor_tensor(out=o_sb[i][:, gs], in0=y_sb[i][:, gs], in1=be_bc[:, gs], op=ALU.add)

        def direct_gain(i):
            vd = GD_FROM.get(i, VDQ[i // 2])
            if vd == 0:
                return
            nc.vector.scalar_tensor_tensor(
                out=y_sb[i][:, 0:vd], in0=y_sb[i][:, 0:vd], scalar=negmu[:, i:i + 1], in1=spread["g"][:, 0:vd], op0=ALU.add,
                op1=ALU.mult,
            )

        def direct_bias(i):
            vd = GD_FROM.get(i, VDQ[i // 2])
            if vd == 0:
                return
            nc.vector.scalar_tensor_tensor(
                out=o_sb[i][:, 0:vd], in0=y_sb[i][:, 0:vd], scalar=rstd[:, i:i + 1], in1=spread["be"][:, 0:vd], op0=ALU.mult,
                op1=ALU.add,
            )
            nc.sync.dma_start(out=o0_view[i][:, 0:vd], in_=o_sb[i][:, 0:vd])

        def direct_absmax(i):
            vd = GD_FROM.get(i, VDQ[i // 2])
            if vd == 0:
                return
            nc.vector.tensor_reduce(
                out=am[:, i * NCH:i * NCH + 1], in_=o_sb[i][:, 0:vd], axis=AX.X, op=ALU.max, apply_absolute_value=True
            )

        def gpsimd_absmax(i):
            nc.vector.tensor_reduce(
                out=am[:, i * NCH + 1:i * NCH + 2], in_=o_sb[i][:, GD_FROM[i]:VDQ[i // 2]], axis=AX.X, op=ALU.max,
                apply_absolute_value=True,
            )

        def gpsimd_store(i):
            gs = slice(GD_FROM[i], VDQ[i // 2])
            nc.sync.dma_start(out=o0_view[i][:, gs], in_=o_sb[i][:, gs])

        def to_features(u, tag):
            q, c = u
            t1_ps[u] = []
            for s in range(2):
                t1 = psum.tile([P, 2, 2, P], F32, name="t1", tag=tag, bufs=4 if tag == "mm" else 2)
                for jj in range(2):
                    c0 = c * CH + (2 * s + jj) * P
                    for e in range(2):
                        nc.tensor.transpose(t1[:, jj, e, :], y_sb[2 * q + e][:, c0:c0 + P], ident[:])
                t1_ps[u].append(t1)

        def gain_bias(u, between=()):
            q, c = u
            ot_sb[u] = []
            for s in range(2):
                ot = late.tile([P, 2, 2, P], F32, name="ot", tag="ot", bufs=8)
                for jj in range(2):
                    j = c * CH // P + 2 * s + jj
                    nc.scalar.activation(
                        out=ot[:, jj, :, :], in_=t1_ps[u][s][:, jj, :, :], func=ACT.Identity,
                        scale=gb_col[:, j:j + 1], bias=gb_col[:, NJ + j:NJ + j + 1],
                    )
                    if 2 * s + jj < len(between):
                        f, i = between[2 * s + jj]
                        f(i)
                ot_sb[u].append(ot)

        def to_tokens(u):
            t2_ps[u] = []
            for e in range(2):
                t2_ps[u].append(psum.tile([P, CH], F32, name="t2", tag="mm", bufs=4))
            for s in range(2):
                for e in range(2):
                    for jj in range(2):
                        k = 2 * s + jj
                        nc.tensor.transpose(t2_ps[u][e][:, k * P:(k + 1) * P], ot_sb[u][s][:, jj, e, :], ident[:])

        def copy_out(u, between=()):
            q, c = u
            for e in range(2):
                i = 2 * q + e
                nc.scalar.copy(out=o_sb[i][:, c * CH:(c + 1) * CH], in_=t2_ps[u][e][:])
                nc.sync.dma_start(out=o0_view[i][:, c * CH:(c + 1) * CH], in_=o_sb[i][:, c * CH:(c + 1) * CH])
                if e < len(between):
                    f, k = between[e]
                    f(k)

        def unit_absmax_early(u):
            q, c = u
            for s in range(2):
                i = 2 * q + s
                nc.vector.tensor_reduce(
                    out=am[:, i * NCH + c:i * NCH + c + 1], in_=ot_sb[u][s][:].rearrange("p a b r -> p (a b r)"), axis=AX.X,
                    op=ALU.max, apply_absolute_value=True,
                )

        def unit_absmax(u):
            q, c = u
            for e in range(2):
                i = 2 * q + e
                nc.vector.tensor_reduce(
                    out=am[:, i * NCH + c:i * NCH + c + 1], in_=o_sb[i][:, c * CH:(c + 1) * CH], axis=AX.X, op=ALU.max,
                    apply_absolute_value=True,
                )

        with tc.tile_pool(name="wpool", bufs=1) as wpool:
            w_raw = []
            wg = []
            for c in range(NCH):
                w_raw.append(wpool.tile([P, 4, CH], BF16, name="w_raw%d" % c))
                wg.append(wpool.tile([P, CH, 4], BF16, name="wg%d" % c, align_bytes=64))
                w_codes.append(keep.tile([P, CH], U32, name="w_codes%d" % c, align_bytes=64))
                w_scales.append(keep.tile([P, CH], U8, name="w_scales%d" % c, align_bytes=64))

            def load_w(c):
                nc.sync.dma_start(out=w_raw[c][:], in_=w_view[:, :, c * CH:(c + 1) * CH])

            def w_interleave(c, eng):
                src = w_raw[c][:].rearrange("p j w -> p w j")
                if eng == "scalar":
                    nc.scalar.copy(out=wg[c][:], in_=src)
                else:
                    nc.vector.tensor_copy(out=wg[c][:], in_=src)

            def w_quantise(c):
                nc.vector.quantize_mx(
                    out=w_codes[c][:].bitcast(FP8X4), scales=w_scales[c][:], in_=wg[c][:].rearrange("p w j -> p (w j)")
                )

            nc.vector.memset(rows[:].bitcast(F32), 0.0)
            nc.vector.memset(ones_b[:], 1.0)
            nc.vector.memset(gb_rows[:], 0.0)
            nc.vector.memset(bc_rows[:], 0.0)
            nc.vector.memset(ones_f[:], 1.0)
            nc.vector.memset(bpart[:], 0.0)
            nc.vector.memset(ones[:], 1.0)
            nc.vector.memset(zeros[:], 0.0)
            nc.vector.memset(am[:], 0.0)
            make_identity(nc, ident[:])
            make_identity(nc, ident_b[:])
            nc.scalar.activation(out=warm[:], in_=ones[:], func=ACT.Abs_reciprocal_sqrt)

            load_x(0)
            load_x(1)
            load_w(0)
            load_w(1)
            load_w(2)
            load_w(3)
            nc.sync.dma_start(out=rows[0:1, 0:D], in_=proj_b.rearrange("(o d) -> o d", o=1))
            load_r(0)
            nc.sync.dma_start(out=bc_rows[0:NJ, :], in_=proj_b.rearrange("(j p) -> j p", p=P))
            for i in range(2, NT):
                load_x(i)
            load_r(1)
            nc.sync.dma_start(out=gb_rows[0:NJ, :], in_=ln_g.rearrange("(j p) -> j p", p=P))
            nc.sync.dma_start(out=gb_rows[NJ:2 * NJ, :], in_=ln_b.rearrange("(j p) -> j p", p=P))
            load_r(3)
            load_r(2)

            x_transpose(0)
            x_copy(0)
            w_interleave(0, "vector")
            x_quantise(0, 1)
            w_interleave(1, "scalar")
            w_quantise(0)

            w_interleave(2, "vector")
            w_interleave(3, "scalar")
            w_quantise(1)
            w_quantise(2)
            project_chunk(0, 0)
            project_chunk(0, 1)
            project_chunk(0, 2)
            add_residual_chunk(0, 0)
            add_residual_chunk(0, 1)
            w_quantise(3)
            add_residual_chunk(0, 2)
            pb = []
            for k in range(2):
                pb.append(psum.tile([P, 2 * CH], BF16, name="pb", tag="t1"))
                for c in range(2):
                    nc.tensor.matmul(
                        out=pb[k][:, c * CH:(c + 1) * CH], lhsT=ones_b[:],
                        rhs=rows[:, (2 * k + c) * CH:(2 * k + c + 1) * CH], start=True, stop=True,
                    )
            nc.tensor.transpose(bct[:, 0:P], bc_rows[:], ident_b[:])
            for a in range(1, NT // 2):
                x_transpose(a)
                x_copy(a)
            project_chunk(0, 3)
            x_quantise(1, 1)
            add_residual_chunk(0, 3)
            x_quantise(2, 1)
            x_quantise(3, 1)
            nc.scalar.activation(out=b_colf[:], in_=bct[:, 0:NJ], func=ACT.Copy, accum_out=bpart[:, 0:1])
            for k in range(2):
                nc.scalar.copy(out=b_bc[:, 2 * k * CH:2 * (k + 1) * CH], in_=pb[k][:])

        late = ctx.enter_context(tc.tile_pool(name="late", bufs=2))

        def sums_of(i):
            project(i)
            add_bias(i, 1)
            if i + R_BUFS < NT:
                load_r(i + R_BUFS)

        units = []
        for q in range(NT // 2):
            for c in range(VDQ[q] // CH, NCH):
                units.append((q, c))
        early = [u for u in units if 2 * u[0] < G_NORM]
        tail = [u for u in units if 2 * u[0] >= G_NORM]

        def direct_step(k):
            if k < 3:
                direct_gain(k)
            if 0 <= k - 1 < NT:
                direct_bias(k - 1)
            if 0 <= k - 3 < len(early):
                unit_absmax(early[k - 3])
            if 3 <= k < NT:
                direct_gain(k)
            if 0 <= k - 2 < NT:
                direct_absmax(k - 2)

        add_bias(0, 2)
        load_r(R_BUFS)
        nc.tensor.matmul(out=bs_ps[:], lhsT=ones_f[:], rhs=bpart[:], start=True, stop=True)
        nc.scalar.activation(out=nbq[:], in_=bs_ps[:, 0:1], func=ACT.Copy, scale=-1.0 / (NCH * D))
        sums_of(1)
        y_sb[PE_TILE] = work.tile([P, D], F32, name="y", tag="y")
        rb_sum(PE_TILE, 0)
        rb_copy(PE_TILE, 0)
        mean_of(0)
        for c in range(NCH):
            project_chunk(2, c)
            add_residual_chunk(2, c)
            if c + 1 < NCH:
                rb_sum(PE_TILE, c + 1)
                rb_copy(PE_TILE, c + 1)
            if c == 0:
                squares_half(0, 0)
        add_bias(2, 1)
        load_r(2 + R_BUFS)
        squares_half(0, 1)
        mean_of(1)
        squares_join(0)
        mean_of(2)
        inv_sd(0)
        shift_of(0)
        normalise(0)
        sums_of(3)
        gbt = psum.tile([P, P], BF16, name="gbt", tag="t1")
        nc.tensor.transpose(gbt[:], gb_rows[:], ident_b[:])
        sums_of(4)
        mean_of(3)
        nc.scalar.copy(out=gb_col[:], in_=gbt[:, 0:2 * NJ])
        nc.scalar.copy(out=gb_colb[:], in_=gbt[:, 0:2 * NJ])
        squares(3)
        squares(1)
        inv_sd(3)
        inv_sd(1)
        shift_of(3)
        shift_of(1)
        normalise(1)
        sums_of(5)
        spread["g"] = cpsum.tile([P, VD], BF16, name="g_ps", tag="g_ps")
        spread["be"] = cpsum.tile([P, VD], BF16, name="be_ps", tag="be_ps")
        for j in range(VD // P):
            nc.tensor.transpose(spread["g"][:, j * P:(j + 1) * P], gb_colb[:, j:j + 1].to_broadcast([P, P]), ident_b[:])
        for j in range(VD // P):
            nc.tensor.transpose(
                spread["be"][:, j * P:(j + 1) * P], gb_colb[:, NJ + j:NJ + j + 1].to_broadcast([P, P]), ident_b[:]
            )
        sums_of(6)
        sums_of(7)
        nc.sync.dma_start(out=g_bc[:], in_=ln_g[0:VD].partition_broadcast(P))
        nc.sync.dma_start(out=be_bc[:], in_=ln_b[0:VD].partition_broadcast(P))
        to_features(early[0], "t1")

        squares(2)
        gain_bias(early[0], ((inv_sd, 2), (shift_of, 2)))
        to_tokens(early[0])
        to_features(early[1], "t1")
        normalise(2)
        copy_out(early[0])

        direct_step(0)
        direct_step(1)
        direct_step(2)
        gain_bias(early[1])
        to_tokens(early[1])
        normalise(3)
        to_features(early[2], "t1")
        copy_out(early[1], ((mean_of, 4),))

        squares(4)
        gain_bias(early[2], ((inv_sd, 4), (mean_of, 5), (shift_of, 4)))
        to_tokens(early[2])
        normalise(4)
        to_features(early[3], "t1")
        direct_step(3)
        direct_step(4)
        squares(5)
        copy_out(early[2], ((inv_sd, 5),))
        gpsimd_direct(5)
        mean_of(6)
        gain_bias(early[3], ((mean_of, 7),))
        to_tokens(early[3])
        direct_step(5)
        squares(6)
        copy_out(early[3], ((inv_sd, 6),))
        direct_step(6)
        squares(7)
        inv_sd(7)
        gpsimd_direct(7)

        n = len(tail)
        for k in range(n + 2):
            if k < n:
                to_features(tail[k], "t1" if k % 2 == 0 else "mm")
            if k == 1:
                gpsimd_store(5)
            if 0 <= k - 1 < n:
                gain_bias(tail[k - 1])
            if k == n:
                gpsimd_store(7)
            if 0 <= k - 2 < n:
                copy_out(tail[k - 2])
            if 0 <= k - 1 < n:
                to_tokens(tail[k - 1])
            if k < 3:
                direct_step(NT - 1 + k)
            if k == 3:
                gpsimd_absmax(5)
            if 0 <= k - 1 < n:
                unit_absmax_early(tail[k - 1])
        gpsimd_absmax(7)

        pm = keep.tile([P, 1], F32, name="pm")
        am_s = keep.tile([P, NT * NCH], F32, name="am_s")
        nc.vector.tensor_scalar(
            out=am_s[:], in0=am[:], scalar1=1.0 / 448.0, scalar2=None, op0=ALU.mult, op1=ALU.max, accum_out=pm[:]
        )
        pt = psum.tile([P, P], F32, name="pt", tag="t1")
        nc.tensor.transpose(pt[:], pm[:, 0:1].to_broadcast([P, P]), ident[:])
        gm = keep.tile([P, 1], F32, name="gm")
        nc.vector.tensor_reduce(out=gm[:], in_=pt[:], axis=AX.X, op=ALU.max)
        fac = keep.tile([P, 1], F32, name="fac")
        nc.vector.reciprocal(out=fac[:], in_=gm[:])

        for i in range(NT):
            f8 = work.tile([P, D], FP8, name="f8", tag="y")
            o = o_sb[i]
            nc.vector.tensor_scalar(
                out=f8[:, 0:CAST_V], in0=o[:, 0:CAST_V], scalar1=fac[:, 0:1], scalar2=None, op0=ALU.mult,
                saturate=False,
            )
            nc.scalar.activation(
                out=f8[:, CAST_V:D], in_=o[:, CAST_V:D], func=ACT.Identity, scale=fac[:, 0:1],
                bias=zeros[:, 0:1], saturate=False,
            )
            nc.sync.dma_start(out=o1_view[i], in_=f8[:].bitcast(U8))
